import numpy as np
import ml_dtypes


def mxq(x, axis, fmt="e4m3"):
    dtype, down = {"e4m3": (ml_dtypes.float8_e4m3fn, 7), "e5m2": (ml_dtypes.float8_e5m2, 14)}[fmt]
    v = np.moveaxis(np.asarray(x, np.float32).astype(ml_dtypes.bfloat16).astype(np.float64), axis, -1)
    blocks = v.reshape(v.shape[:-1] + (-1, 32))
    amax = np.abs(blocks).max(-1, keepdims=True)
    byte = np.maximum(np.where(amax > 0, np.frexp(amax)[1] - 1 + 127, 0) - down, 1)
    scale = np.exp2(byte - 127.0)
    codes = (blocks / scale).astype(np.float32).astype(dtype).astype(np.float64)
    return np.moveaxis((codes * scale).reshape(v.shape), -1, axis)


WIDE = False


def mx_kscale(k):
    if not WIDE:
        return np.ones(k)
    levels = np.array([10, -10, 5, -5, 0])
    a = np.random.permutation(np.resize(levels, k // 512 * 4)).reshape(k // 512, 4)
    idx = np.arange(k)
    return np.exp2(a[idx // 512, idx % 128 // 32])


BF16 = ml_dtypes.bfloat16


def bf(x):
    return np.asarray(x, np.float32).astype(BF16)


def f64(x):
    return np.asarray(x).astype(np.float64)


B, S, D_MODEL, D_POS, H, D_FF = 512, 2, 1024, 512, 4, 2048
DPP = D_POS // H
DPH = D_MODEL // H


def setup_inputs():
    s = mx_kscale(D_MODEL)
    gq = np.exp2(np.random.uniform(-1.0, 1.0, (S, H, B, 1)))
    gk = np.exp2(np.random.uniform(-1.0, 1.0, (S, H, B, 1)))
    return {"q_pos": bf(np.random.standard_normal((S, H, B, DPP)) * gq * 3.0 / np.sqrt(DPP)),
            "k_pos": bf(np.random.standard_normal((S, H, B, DPP)) * gk * 3.0 / np.sqrt(DPP)),
            "x_grp": bf(np.random.standard_normal((S, B, D_MODEL)) * s),
            "Wv": bf(np.random.standard_normal((D_MODEL, D_MODEL)) * 0.5 / np.sqrt(D_MODEL) / s),
            "bv": bf(np.random.standard_normal(D_MODEL) * 10.0 / B)}


def reference(q_pos, k_pos, x_grp, Wv, bv):
    v = (mxq(f64(x_grp), 2, "e4m3") @ mxq(f64(Wv).T, 0, "e4m3")) + f64(bv)
    v = v.reshape(S, B, H, DPH).transpose(0, 2, 1, 3)
    q2 = np.sum(f64(q_pos) * f64(q_pos), axis=-1)
    k2 = np.sum(f64(k_pos) * f64(k_pos), axis=-1)
    d2 = q2[..., :, None] + k2[..., None, :] - 2.0 * (f64(q_pos) @ f64(k_pos).transpose(0, 1, 3, 2))
    dist = np.sqrt(np.maximum(d2, 1e-12)) + 1.0
    scores = 1.0 / dist
    causal = np.triu(np.ones((B, B), bool), k=1)
    scores = np.where(causal, 0.0, scores)
    o = mxq(scores, 3, "e4m3") @ mxq(v, 2, "e4m3")
    return o.transpose(0, 2, 1, 3).reshape(S, B, D_MODEL)

@@ -1,0 +1,341 @@
+from contextlib import ExitStack
+
+import concourse.mybir as mybir
+from concourse.masks import make_identity
+
+F32 = mybir.dt.float32
+BF16 = mybir.dt.bfloat16
+U32 = mybir.dt.uint32
+U8 = mybir.dt.uint8
+I32 = mybir.dt.int32
+FP8X4 = mybir.dt.float8_e4m3fn_x4
+ALU = mybir.AluOpType
+ACT = mybir.ActivationFunctionType
+AX = mybir.AxisListType
+
+P = 128
+PACK = 4
+S, H, B = 2, 4, 512
+DPP = 128
+D = 1024
+DPH = D // H
+NT = B // P
+PASSES = D // (P * PACK)
+NW = D // P
+PIECES = 3
+EXTRA = 2 * PIECES
+D2_FLOOR = 1e-12
+D2_CEIL = 2.0**64
+MASKED_LOG = 1e30
+
+FLOPS = 2 * S * B * D * D + 2 * S * H * B * B * DPP + 2 * S * H * B * B * DPH
+
+
+def first_column(i):
+    return P * (i * (i + 1) // 2)
+
+
+def query_tile(head, i):
+    return head[:, first_column(i) : first_column(i + 1)].rearrange("p (b t) -> p b t", t=i + 1)
+
+
+def tile_networklayer_pb_kernel(tc, q_pos, k_pos, x_grp, Wv, bv, out):
+    nc = tc.nc
+    with ExitStack() as ctx:
+        keep = ctx.enter_context(tc.tile_pool(name="keep", bufs=1))
+        logs = ctx.enter_context(tc.tile_pool(name="logs", bufs=S * H))
+        small = ctx.enter_context(tc.tile_pool(name="small", bufs=2))
+        stage = ctx.enter_context(tc.tile_pool(name="stage", bufs=3))
+        psum_t = ctx.enter_context(tc.psum_pool(name="psum_t", bufs=2))
+        psum_d = ctx.enter_context(tc.psum_pool(name="psum_d", bufs=3))
+        psum_m = ctx.enter_context(tc.psum_pool(name="psum_m", bufs=3))
+        ctx.enter_context(tc.manual_schedule())
+
+        q_nat = [keep.tile([P, H, NT, DPP], BF16, name="q_nat%d" % s) for s in range(S)]
+        k_nat = [keep.tile([P, H, NT, DPP], BF16, name="k_nat%d" % s) for s in range(S)]
+        w_nat = keep.tile([P, NW, D], BF16)
+        x_nat = [keep.tile([P, NT, D], BF16, name="x_nat%d" % s) for s in range(S)]
+        bias = keep.tile([P, D], BF16)
+        for s in range(S):
+            nc.sync.dma_start(out=q_nat[s][:], in_=q_pos[s].rearrange("h (i p) f -> p h i f", p=P))
+            nc.sync.dma_start(out=k_nat[s][:], in_=k_pos[s].rearrange("h (i p) f -> p h i f", p=P))
+        w_rows = Wv.rearrange("(j p) k -> p j k", p=P)
+        for half in range(2):
+            rows = slice(half * NW // 2, (half + 1) * NW // 2)
+            nc.sync.dma_start(out=w_nat[:, rows, :], in_=w_rows[:, rows, :])
+        for s in range(S):
+            nc.sync.dma_start(out=x_nat[s][:], in_=x_grp[s].rearrange("(t p) k -> p t k", p=P))
+        nc.sync.dma_start(out=bias[:], in_=bv.partition_broadcast(P))
+
+        ident_bf = keep.tile([P, P], BF16)
+        make_identity(nc, ident_bf[:])
+        ident_f32 = keep.tile([P, P], F32)
+        make_identity(nc, ident_f32[:])
+        one = keep.tile([P, 1], F32)
+        nc.vector.memset(one[:], 1.0)
+        nc.scalar.activation(out=one[:], in_=one[:], func=ACT.Ln)
+        above = keep.tile([P, P], F32)
+        nc.gpsimd.memset(above[:], 0.0)
+        nc.gpsimd.affine_select(
+            out=above[:],
+            in_=above[:],
+            pattern=[[1, P]],
+            compare_op=ALU.is_ge,
+            fill=MASKED_LOG,
+            base=0,
+            channel_multiplier=-1,
+        )
+        causal = keep.tile([P, first_column(NT)], F32)
+        nc.gpsimd.memset(causal[:], 0.0)
+        for i in range(NT):
+            nc.gpsimd.tensor_copy(out=query_tile(causal, i)[:, :, i], in_=above[:])
+
+        q_feat = [keep.tile([P, NT, P], BF16, name="q_feat%d" % s) for s in range(S)]
+        k_feat = [keep.tile([P, NT, P], BF16, name="k_feat%d" % s) for s in range(S)]
+
+        def by_head(feat):
+            return feat[:, :, 0 : H * EXTRA].rearrange("p i (h j) -> p i h j", j=EXTRA)
+
+        for s in range(S):
+            nc.vector.memset(q_feat[s][:], 0.0)
+            nc.vector.memset(by_head(q_feat[s])[:, :, :, PIECES:EXTRA], 1.0)
+            nc.vector.memset(k_feat[s][:], 0.0)
+            nc.vector.memset(by_head(k_feat[s])[:, :, :, 0:PIECES], 1.0)
+
+        w_bf = [
+            keep.tile([P, NT, P, PACK], BF16, name="w_bf%d" % n, align_bytes=64) for n in range(S * H)
+        ]
+        for n in range(S * H):
+            nc.vector.memset(w_bf[n][:].rearrange("p i b t -> p (i b t)").bitcast(I32), 0)
+        head_rows = keep.tile([P, H], F32)
+        nc.vector.tensor_reduce(
+            out=head_rows[:],
+            in_=ident_f32[:, 0 : H * EXTRA].rearrange("p (h j) -> p h j", j=EXTRA),
+            axis=AX.X,
+            op=ALU.add,
+        )
+
+        qT = keep.tile([P, S, H, B], BF16)
+        kT = keep.tile([P, S, H, B], BF16)
+        q_extra = keep.tile([P, S, B], BF16)
+        k_extra = keep.tile([P, S, H, B], BF16)
+        square = keep.tile([P, DPP], BF16)
+
+        def sums_of_squares(nat, name):
+            sums = keep.tile([P, H * NT], F32, name=name)
+            for h in range(H):
+                for i in range(NT):
+                    n = h * NT + i
+                    nc.scalar.activation(
+                        out=square[:], in_=nat[:, h, i, :], func=ACT.Square, accum_out=sums[:, n : n + 1]
+                    )
+            return sums
+
+        def transposed(blocks):
+            tp = psum_t.tile([P, NT, P], BF16, tag="tp")
+            for i in range(NT):
+                nc.tensor.transpose(tp[:, i, :], blocks[:, i, :], ident_bf[:])
+            return tp[:].rearrange("p i b -> p (i b)")
+
+        def transpose_queries(s):
+            for h in range(H):
+                nc.vector.tensor_scalar(
+                    out=qT[:, s, h, :], in0=transposed(q_nat[s][:, h]), scalar1=-2.0, scalar2=None, op0=ALU.mult
+                )
+
+        def transpose_keys(s):
+            for h in range(H):
+                nc.vector.tensor_copy(out=kT[:, s, h, :], in_=transposed(k_nat[s][:, h]))
+
+        def split_in_pieces(sums, feat, first):
+            rest = sums[:].rearrange("p (h i) -> p i h", i=NT)
+            for j in range(PIECES):
+                piece = by_head(feat)[:, :, :, first + j]
+                nc.vector.tensor_copy(out=piece, in_=rest)
+                if j < PIECES - 1:
+                    left = small.tile([P, NT, H], F32, tag="left")
+                    nc.vector.tensor_tensor(out=left[:], in0=rest, in1=piece, op=ALU.subtract)
+                    rest = left[:]
+
+        def transpose_extra_features(s):
+            nc.vector.tensor_copy(out=q_extra[:, s, :], in_=transposed(q_feat[s]))
+            k_rows = transposed(k_feat[s])
+            for h in range(H):
+                nc.vector.tensor_scalar(
+                    out=k_extra[:, s, h, :], in0=k_rows, scalar1=head_rows[:, h : h + 1], scalar2=None, op0=ALU.mult
+                )
+
+        xw_codes = keep.tile([P, NW + S * NT, PASSES, P], U32, align_bytes=64)
+        xw_scales = keep.tile([P, NW + S * NT, PASSES, P], U8, align_bytes=64)
+
+        def row_tile(n):
+            if n < NW:
+                return w_nat[:, n, :]
+            return x_nat[(n - NW) // NT][:, (n - NW) % NT, :]
+
+        def transpose_rows(pair):
+            grouped = stage.tile([P, 2 * PASSES * P * PACK], BF16, tag="grouped", align_bytes=64)
+            words = grouped[:].bitcast(F32).rearrange("p (n g r u) -> p n g r u", n=2, g=PASSES, u=2)
+            for n in range(2):
+                source = row_tile(2 * pair + n).bitcast(F32)
+                tp = psum_t.tile([P, PASSES, 2, P], F32, tag="tp")
+                for g in range(PASSES):
+                    for u in range(2):
+                        first = (2 * g + u) * P
+                        nc.tensor.transpose(tp[:, g, u, :], source[:, first : first + P], ident_f32[:])
+                nc.scalar.copy(out=words[:, n], in_=tp[:].rearrange("p g u r -> p g r u"))
+            return grouped
+
+        def quantise_rows(pair, grouped):
+            tiles = slice(2 * pair, 2 * pair + 2)
+            nc.vector.quantize_mx(
+                out=xw_codes[:, tiles].rearrange("p n g r -> p (n g r)").bitcast(FP8X4),
+                scales=xw_scales[:, tiles].rearrange("p n g r -> p (n g r)"),
+                in_=grouped[:],
+            )
+
+        def distances(s, h):
+            logd = logs.tile([P, first_column(NT)], F32, tag="logd")
+            for i in range(NT):
+                d2 = psum_d.tile([P, NT, P], F32, tag="d2")
+                b_cols = slice(i * P, (i + 1) * P)
+                for t in range(i + 1):
+                    c_cols = slice(t * P, (t + 1) * P)
+                    nc.tensor.matmul(
+                        out=d2[:, t, :], lhsT=kT[:, s, h, c_cols], rhs=qT[:, s, h, b_cols], start=True, stop=False
+                    )
+                    nc.tensor.matmul(
+                        out=d2[:, t, :], lhsT=k_extra[:, s, h, c_cols], rhs=q_extra[:, s, b_cols], start=False, stop=True
+                    )
+                nc.vector.tensor_scalar(
+                    out=query_tile(logd, i),
+                    in0=d2[:, 0 : i + 1, :].rearrange("p t b -> p b t"),
+                    scalar1=D2_FLOOR,
+                    scalar2=D2_CEIL,
+                    op0=ALU.max,
+                    op1=ALU.min,
+                )
+            return logd
+
+        def logarithms(logd):
+            nc.scalar.activation(out=logd[:], in_=logd[:], func=ACT.Ln)
+            nc.gpsimd.tensor_tensor(out=logd[:], in0=logd[:], in1=causal[:], op=ALU.add)
+
+        v_codes = keep.tile([P, S, D], U32, align_bytes=64)
+        v_scales = keep.tile([P, S, D], U8, align_bytes=64)
+        CHUNKS = 4
+
+        def project_values(s, part):
+            v_bf = stage.tile([P, CHUNKS, P, PACK], BF16, tag="v_bf", bufs=2, align_bytes=64)
+            for n in range(CHUNKS):
+                j = part * CHUNKS + n
+                v_ps = psum_m.tile([P, NT, P], F32, tag="mx")
+                for t in range(NT):
+                    for g in range(PASSES):
+                        nc.tensor.matmul_mx(
+                            out=v_ps[:, t, :],
+                            lhsT=xw_codes[:, NW + NT * s + t, g, :].bitcast(FP8X4),
+                            lhsT_scale=xw_scales[:, NW + NT * s + t, g, :],
+                            rhs=xw_codes[:, j, g, :].bitcast(FP8X4),
+                            rhs_scale=xw_scales[:, j, g, :],
+                            start=(g == 0),
+                            stop=(g == PASSES - 1),
+                        )
+                nc.vector.tensor_tensor(
+                    out=v_bf[:, n],
+                    in0=v_ps[:].rearrange("p t d -> p d t"),
+                    in1=bias[:, j * P : (j + 1) * P].unsqueeze(2).to_broadcast([P, P, PACK]),
+                    op=ALU.add,
+                )
+            cols = slice(part * CHUNKS * P, (part + 1) * CHUNKS * P)
+            nc.vector.quantize_mx(
+                out=v_codes[:, s, cols].bitcast(FP8X4),
+                scales=v_scales[:, s, cols],
+                in_=v_bf[:].rearrange("p n d t -> p (n d t)"),
+            )
+
+        def weights(n, logd):
+            for i in range(NT):
+                nc.scalar.activation(
+                    out=w_bf[n][:, i, :, 0 : i + 1], in_=query_tile(logd, i), func=ACT.Sigmoid, scale=-0.5
+                )
+
+        def multiply(s, h):
+            n = s * H + h
+            w_codes = stage.tile([P, NT * P], U32, tag="w_codes", align_bytes=64)
+            w_scales = stage.tile([P, NT * P], U8, tag="w_scales", align_bytes=64)
+            nc.vector.quantize_mx(
+                out=w_codes[:].bitcast(FP8X4), scales=w_scales[:], in_=w_bf[n][:].rearrange("p i b t -> p (i b t)")
+            )
+            d_cols = slice(h * DPH, (h + 1) * DPH)
+            banks = []
+            for pair in range(NT // 2):
+                o_ps = psum_d.tile([P, 2, DPH], F32, tag="d2")
+                for e in range(2):
+                    b_cols = slice((2 * pair + e) * P, (2 * pair + e + 1) * P)
+                    nc.tensor.matmul_mx(
+                        out=o_ps[:, e, :],
+                        lhsT=w_codes[:, b_cols].bitcast(FP8X4),
+                        lhsT_scale=w_scales[:, b_cols],
+                        rhs=v_codes[:, s, d_cols].bitcast(FP8X4),
+                        rhs_scale=v_scales[:, s, d_cols],
+                        start=True,
+                        stop=True,
+                    )
+                banks.append(o_ps)
+            return banks
+
+        def store(s, h, banks):
+            o_sb = stage.tile([P, NT, DPH], F32, tag="o_sb")
+            nc.vector.tensor_copy(out=o_sb[:, 0:2, :], in_=banks[0][:])
+            if h % 2 == 1:
+                nc.scalar.copy(out=o_sb[:, 2:4, :], in_=banks[1][:])
+            else:
+                nc.vector.tensor_copy(out=o_sb[:, 2:4, :], in_=banks[1][:])
+            d_cols = slice(h * DPH, (h + 1) * DPH)
+            nc.sync.dma_start(out=out[s].rearrange("(i p) d -> p i d", p=P)[:, :, d_cols], in_=o_sb[:])
+
+        HEADS = S * H
+        PARTS = NW // CHUNKS
+        q_sums = [sums_of_squares(q_nat[0], "q_sums0")]
+        k_sums = [sums_of_squares(k_nat[0], "k_sums0")]
+        q_sums.append(sums_of_squares(q_nat[1], "q_sums1"))
+        k_sums.append(sums_of_squares(k_nat[1], "k_sums1"))
+
+        def split_sums(s):
+            split_in_pieces(q_sums[s], q_feat[s], 0)
+            split_in_pieces(k_sums[s], k_feat[s], PIECES)
+
+        transpose_queries(0)
+        transpose_keys(0)
+        transpose_queries(1)
+        split_sums(0)
+        transpose_keys(1)
+        transpose_extra_features(0)
+
+        head_logs = []
+        row_pairs = []
+        for n in range(HEADS):
+            head_logs.append(distances(n // H, n % H))
+            if n == 0:
+                split_sums(1)
+            if n == 1:
+                transpose_extra_features(1)
+            row_pairs.append(transpose_rows(n))
+            logarithms(head_logs[n])
+            if n > 0:
+                quantise_rows(n - 1, row_pairs[n - 1])
+        quantise_rows(HEADS - 1, row_pairs[HEADS - 1])
+
+        for part in range(PARTS):
+            project_values(0, part)
+        head_banks = []
+        for n in range(HEADS + 2):
+            if n < HEADS:
+                weights(n, head_logs[n])
+            if n >= 2:
+                store((n - 2) // H, (n - 2) % H, head_banks[n - 2])
+            if 1 <= n <= HEADS:
+                head_banks.append(multiply((n - 1) // H, (n - 1) % H))
+            if 2 <= n < 2 + PARTS:
+                project_values(1, n - 2)

@@ -7,7 +7,6 @@ F32 = mybir.dt.float32
 BF16 = mybir.dt.bfloat16
 U32 = mybir.dt.uint32
 U8 = mybir.dt.uint8
-I32 = mybir.dt.int32
 FP8X4 = mybir.dt.float8_e4m3fn_x4
 ALU = mybir.AluOpType
 ACT = mybir.ActivationFunctionType
@@ -22,6 +21,8 @@ DPH = D // H
 NT = B // P
 PASSES = D // (P * PACK)
 NW = D // P
+HEADS = S * H
+CHUNKS = 4
 PIECES = 3
 EXTRA = 2 * PIECES
 D2_FLOOR = 1e-12
@@ -36,306 +37,302 @@ def first_column(i):
 
 
 def query_tile(head, i):
-    return head[:, first_column(i) : first_column(i + 1)].rearrange("p (b t) -> p b t", t=i + 1)
+    return head[:, first_column(i) : first_column(i + 1)].rearrange("p (t b) -> p t b", t=i + 1)
 
 
 def tile_networklayer_pb_kernel(tc, q_pos, k_pos, x_grp, Wv, bv, out):
     nc = tc.nc
     with ExitStack() as ctx:
         keep = ctx.enter_context(tc.tile_pool(name="keep", bufs=1))
-        logs = ctx.enter_context(tc.tile_pool(name="logs", bufs=S * H))
-        small = ctx.enter_context(tc.tile_pool(name="small", bufs=2))
+        logs = ctx.enter_context(tc.tile_pool(name="logs", bufs=HEADS))
         stage = ctx.enter_context(tc.tile_pool(name="stage", bufs=3))
         psum_t = ctx.enter_context(tc.psum_pool(name="psum_t", bufs=2))
         psum_d = ctx.enter_context(tc.psum_pool(name="psum_d", bufs=3))
         psum_m = ctx.enter_context(tc.psum_pool(name="psum_m", bufs=3))
         ctx.enter_context(tc.manual_schedule())
 
-        q_nat = [keep.tile([P, H, NT, DPP], BF16, name="q_nat%d" % s) for s in range(S)]
-        k_nat = [keep.tile([P, H, NT, DPP], BF16, name="k_nat%d" % s) for s in range(S)]
-        w_nat = keep.tile([P, NW, D], BF16)
-        x_nat = [keep.tile([P, NT, D], BF16, name="x_nat%d" % s) for s in range(S)]
         bias = keep.tile([P, D], BF16)
-        for s in range(S):
-            nc.sync.dma_start(out=q_nat[s][:], in_=q_pos[s].rearrange("h (i p) f -> p h i f", p=P))
-            nc.sync.dma_start(out=k_nat[s][:], in_=k_pos[s].rearrange("h (i p) f -> p h i f", p=P))
-        w_rows = Wv.rearrange("(j p) k -> p j k", p=P)
-        for half in range(2):
-            rows = slice(half * NW // 2, (half + 1) * NW // 2)
-            nc.sync.dma_start(out=w_nat[:, rows, :], in_=w_rows[:, rows, :])
-        for s in range(S):
-            nc.sync.dma_start(out=x_nat[s][:], in_=x_grp[s].rearrange("(t p) k -> p t k", p=P))
-        nc.sync.dma_start(out=bias[:], in_=bv.partition_broadcast(P))
-
-        ident_bf = keep.tile([P, P], BF16)
-        make_identity(nc, ident_bf[:])
-        ident_f32 = keep.tile([P, P], F32)
-        make_identity(nc, ident_f32[:])
-        one = keep.tile([P, 1], F32)
-        nc.vector.memset(one[:], 1.0)
-        nc.scalar.activation(out=one[:], in_=one[:], func=ACT.Ln)
-        above = keep.tile([P, P], F32)
-        nc.gpsimd.memset(above[:], 0.0)
-        nc.gpsimd.affine_select(
-            out=above[:],
-            in_=above[:],
-            pattern=[[1, P]],
-            compare_op=ALU.is_ge,
-            fill=MASKED_LOG,
-            base=0,
-            channel_multiplier=-1,
-        )
-        causal = keep.tile([P, first_column(NT)], F32)
-        nc.gpsimd.memset(causal[:], 0.0)
-        for i in range(NT):
-            nc.gpsimd.tensor_copy(out=query_tile(causal, i)[:, :, i], in_=above[:])
-
-        q_feat = [keep.tile([P, NT, P], BF16, name="q_feat%d" % s) for s in range(S)]
-        k_feat = [keep.tile([P, NT, P], BF16, name="k_feat%d" % s) for s in range(S)]
-
-        def by_head(feat):
-            return feat[:, :, 0 : H * EXTRA].rearrange("p i (h j) -> p i h j", j=EXTRA)
-
-        for s in range(S):
-            nc.vector.memset(q_feat[s][:], 0.0)
-            nc.vector.memset(by_head(q_feat[s])[:, :, :, PIECES:EXTRA], 1.0)
-            nc.vector.memset(k_feat[s][:], 0.0)
-            nc.vector.memset(by_head(k_feat[s])[:, :, :, 0:PIECES], 1.0)
-
-        w_bf = [
-            keep.tile([P, NT, P, PACK], BF16, name="w_bf%d" % n, align_bytes=64) for n in range(S * H)
-        ]
-        for n in range(S * H):
-            nc.vector.memset(w_bf[n][:].rearrange("p i b t -> p (i b t)").bitcast(I32), 0)
-        head_rows = keep.tile([P, H], F32)
-        nc.vector.tensor_reduce(
-            out=head_rows[:],
-            in_=ident_f32[:, 0 : H * EXTRA].rearrange("p (h j) -> p h j", j=EXTRA),
-            axis=AX.X,
-            op=ALU.add,
-        )
-
-        qT = keep.tile([P, S, H, B], BF16)
-        kT = keep.tile([P, S, H, B], BF16)
-        q_extra = keep.tile([P, S, B], BF16)
-        k_extra = keep.tile([P, S, H, B], BF16)
-        square = keep.tile([P, DPP], BF16)
-
-        def sums_of_squares(nat, name):
-            sums = keep.tile([P, H * NT], F32, name=name)
-            for h in range(H):
-                for i in range(NT):
-                    n = h * NT + i
-                    nc.scalar.activation(
-                        out=square[:], in_=nat[:, h, i, :], func=ACT.Square, accum_out=sums[:, n : n + 1]
-                    )
-            return sums
-
-        def transposed(blocks):
-            tp = psum_t.tile([P, NT, P], BF16, tag="tp")
-            for i in range(NT):
-                nc.tensor.transpose(tp[:, i, :], blocks[:, i, :], ident_bf[:])
-            return tp[:].rearrange("p i b -> p (i b)")
-
-        def transpose_queries(s):
-            for h in range(H):
-                nc.vector.tensor_scalar(
-                    out=qT[:, s, h, :], in0=transposed(q_nat[s][:, h]), scalar1=-2.0, scalar2=None, op0=ALU.mult
-                )
-
-        def transpose_keys(s):
-            for h in range(H):
-                nc.vector.tensor_copy(out=kT[:, s, h, :], in_=transposed(k_nat[s][:, h]))
-
-        def split_in_pieces(sums, feat, first):
-            rest = sums[:].rearrange("p (h i) -> p i h", i=NT)
-            for j in range(PIECES):
-                piece = by_head(feat)[:, :, :, first + j]
-                nc.vector.tensor_copy(out=piece, in_=rest)
-                if j < PIECES - 1:
-                    left = small.tile([P, NT, H], F32, tag="left")
-                    nc.vector.tensor_tensor(out=left[:], in0=rest, in1=piece, op=ALU.subtract)
-                    rest = left[:]
-
-        def transpose_extra_features(s):
-            nc.vector.tensor_copy(out=q_extra[:, s, :], in_=transposed(q_feat[s]))
-            k_rows = transposed(k_feat[s])
-            for h in range(H):
-                nc.vector.tensor_scalar(
-                    out=k_extra[:, s, h, :], in0=k_rows, scalar1=head_rows[:, h : h + 1], scalar2=None, op0=ALU.mult
-                )
-
         xw_codes = keep.tile([P, NW + S * NT, PASSES, P], U32, align_bytes=64)
         xw_scales = keep.tile([P, NW + S * NT, PASSES, P], U8, align_bytes=64)
-
-        def row_tile(n):
-            if n < NW:
-                return w_nat[:, n, :]
-            return x_nat[(n - NW) // NT][:, (n - NW) % NT, :]
-
-        def transpose_rows(pair):
-            grouped = stage.tile([P, 2 * PASSES * P * PACK], BF16, tag="grouped", align_bytes=64)
-            words = grouped[:].bitcast(F32).rearrange("p (n g r u) -> p n g r u", n=2, g=PASSES, u=2)
-            for n in range(2):
-                source = row_tile(2 * pair + n).bitcast(F32)
-                tp = psum_t.tile([P, PASSES, 2, P], F32, tag="tp")
-                for g in range(PASSES):
-                    for u in range(2):
-                        first = (2 * g + u) * P
-                        nc.tensor.transpose(tp[:, g, u, :], source[:, first : first + P], ident_f32[:])
-                nc.scalar.copy(out=words[:, n], in_=tp[:].rearrange("p g u r -> p g r u"))
-            return grouped
-
-        def quantise_rows(pair, grouped):
-            tiles = slice(2 * pair, 2 * pair + 2)
-            nc.vector.quantize_mx(
-                out=xw_codes[:, tiles].rearrange("p n g r -> p (n g r)").bitcast(FP8X4),
-                scales=xw_scales[:, tiles].rearrange("p n g r -> p (n g r)"),
-                in_=grouped[:],
-            )
-
-        def distances(s, h):
-            logd = logs.tile([P, first_column(NT)], F32, tag="logd")
-            for i in range(NT):
-                d2 = psum_d.tile([P, NT, P], F32, tag="d2")
-                b_cols = slice(i * P, (i + 1) * P)
-                for t in range(i + 1):
-                    c_cols = slice(t * P, (t + 1) * P)
-                    nc.tensor.matmul(
-                        out=d2[:, t, :], lhsT=kT[:, s, h, c_cols], rhs=qT[:, s, h, b_cols], start=True, stop=False
-                    )
-                    nc.tensor.matmul(
-                        out=d2[:, t, :], lhsT=k_extra[:, s, h, c_cols], rhs=q_extra[:, s, b_cols], start=False, stop=True
-                    )
-                nc.vector.tensor_scalar(
-                    out=query_tile(logd, i),
-                    in0=d2[:, 0 : i + 1, :].rearrange("p t b -> p b t"),
-                    scalar1=D2_FLOOR,
-                    scalar2=D2_CEIL,
-                    op0=ALU.max,
-                    op1=ALU.min,
-                )
-            return logd
-
-        def logarithms(logd):
-            nc.scalar.activation(out=logd[:], in_=logd[:], func=ACT.Ln)
-            nc.gpsimd.tensor_tensor(out=logd[:], in0=logd[:], in1=causal[:], op=ALU.add)
-
         v_codes = keep.tile([P, S, D], U32, align_bytes=64)
         v_scales = keep.tile([P, S, D], U8, align_bytes=64)
-        CHUNKS = 4
-
-        def project_values(s, part):
-            v_bf = stage.tile([P, CHUNKS, P, PACK], BF16, tag="v_bf", bufs=2, align_bytes=64)
-            for n in range(CHUNKS):
-                j = part * CHUNKS + n
-                v_ps = psum_m.tile([P, NT, P], F32, tag="mx")
-                for t in range(NT):
-                    for g in range(PASSES):
-                        nc.tensor.matmul_mx(
-                            out=v_ps[:, t, :],
-                            lhsT=xw_codes[:, NW + NT * s + t, g, :].bitcast(FP8X4),
-                            lhsT_scale=xw_scales[:, NW + NT * s + t, g, :],
-                            rhs=xw_codes[:, j, g, :].bitcast(FP8X4),
-                            rhs_scale=xw_scales[:, j, g, :],
-                            start=(g == 0),
-                            stop=(g == PASSES - 1),
-                        )
-                nc.vector.tensor_tensor(
-                    out=v_bf[:, n],
-                    in0=v_ps[:].rearrange("p t d -> p d t"),
-                    in1=bias[:, j * P : (j + 1) * P].unsqueeze(2).to_broadcast([P, P, PACK]),
-                    op=ALU.add,
-                )
-            cols = slice(part * CHUNKS * P, (part + 1) * CHUNKS * P)
-            nc.vector.quantize_mx(
-                out=v_codes[:, s, cols].bitcast(FP8X4),
-                scales=v_scales[:, s, cols],
-                in_=v_bf[:].rearrange("p n d t -> p (n d t)"),
-            )
-
-        def weights(n, logd):
-            for i in range(NT):
-                nc.scalar.activation(
-                    out=w_bf[n][:, i, :, 0 : i + 1], in_=query_tile(logd, i), func=ACT.Sigmoid, scale=-0.5
-                )
-
-        def multiply(s, h):
-            n = s * H + h
-            w_codes = stage.tile([P, NT * P], U32, tag="w_codes", align_bytes=64)
-            w_scales = stage.tile([P, NT * P], U8, tag="w_scales", align_bytes=64)
-            nc.vector.quantize_mx(
-                out=w_codes[:].bitcast(FP8X4), scales=w_scales[:], in_=w_bf[n][:].rearrange("p i b t -> p (i b t)")
-            )
-            d_cols = slice(h * DPH, (h + 1) * DPH)
-            banks = []
-            for pair in range(NT // 2):
-                o_ps = psum_d.tile([P, 2, DPH], F32, tag="d2")
-                for e in range(2):
-                    b_cols = slice((2 * pair + e) * P, (2 * pair + e + 1) * P)
-                    nc.tensor.matmul_mx(
-                        out=o_ps[:, e, :],
-                        lhsT=w_codes[:, b_cols].bitcast(FP8X4),
-                        lhsT_scale=w_scales[:, b_cols],
-                        rhs=v_codes[:, s, d_cols].bitcast(FP8X4),
-                        rhs_scale=v_scales[:, s, d_cols],
-                        start=True,
-                        stop=True,
-                    )
-                banks.append(o_ps)
-            return banks
-
-        def store(s, h, banks):
-            o_sb = stage.tile([P, NT, DPH], F32, tag="o_sb")
-            nc.vector.tensor_copy(out=o_sb[:, 0:2, :], in_=banks[0][:])
-            if h % 2 == 1:
-                nc.scalar.copy(out=o_sb[:, 2:4, :], in_=banks[1][:])
-            else:
-                nc.vector.tensor_copy(out=o_sb[:, 2:4, :], in_=banks[1][:])
-            d_cols = slice(h * DPH, (h + 1) * DPH)
-            nc.sync.dma_start(out=out[s].rearrange("(i p) d -> p i d", p=P)[:, :, d_cols], in_=o_sb[:])
-
-        HEADS = S * H
-        PARTS = NW // CHUNKS
-        q_sums = [sums_of_squares(q_nat[0], "q_sums0")]
-        k_sums = [sums_of_squares(k_nat[0], "k_sums0")]
-        q_sums.append(sums_of_squares(q_nat[1], "q_sums1"))
-        k_sums.append(sums_of_squares(k_nat[1], "k_sums1"))
-
-        def split_sums(s):
-            split_in_pieces(q_sums[s], q_feat[s], 0)
-            split_in_pieces(k_sums[s], k_feat[s], PIECES)
-
-        transpose_queries(0)
-        transpose_keys(0)
-        transpose_queries(1)
-        split_sums(0)
-        transpose_keys(1)
-        transpose_extra_features(0)
-
+        w_bf = [keep.tile([P, NT, P, PACK], BF16, name="w_bf%d" % n, align_bytes=64) for n in range(HEADS)]
         head_logs = []
-        row_pairs = []
-        for n in range(HEADS):
-            head_logs.append(distances(n // H, n % H))
-            if n == 0:
-                split_sums(1)
-            if n == 1:
-                transpose_extra_features(1)
-            row_pairs.append(transpose_rows(n))
-            logarithms(head_logs[n])
-            if n > 0:
-                quantise_rows(n - 1, row_pairs[n - 1])
-        quantise_rows(HEADS - 1, row_pairs[HEADS - 1])
 
-        for part in range(PARTS):
-            project_values(0, part)
-        head_banks = []
-        for n in range(HEADS + 2):
-            if n < HEADS:
-                weights(n, head_logs[n])
-            if n >= 2:
-                store((n - 2) // H, (n - 2) % H, head_banks[n - 2])
-            if 1 <= n <= HEADS:
-                head_banks.append(multiply((n - 1) // H, (n - 1) % H))
-            if 2 <= n < 2 + PARTS:
-                project_values(1, n - 2)
+        with tc.tile_pool(name="inputs", bufs=1) as inputs, tc.tile_pool(name="small", bufs=2) as small:
+            q_nat = [inputs.tile([P, H, NT, DPP], BF16, name="q_nat%d" % s) for s in range(S)]
+            k_nat = [inputs.tile([P, H, NT, DPP], BF16, name="k_nat%d" % s) for s in range(S)]
+            w_nat = inputs.tile([P, NW, D], BF16)
+            x_nat = [inputs.tile([P, NT, D], BF16, name="x_nat%d" % s) for s in range(S)]
+            for s in range(S):
+                nc.sync.dma_start(out=q_nat[s][:], in_=q_pos[s].rearrange("h (i p) f -> p h i f", p=P))
+                nc.sync.dma_start(out=k_nat[s][:], in_=k_pos[s].rearrange("h (i p) f -> p h i f", p=P))
+            w_rows = Wv.rearrange("(j p) k -> p j k", p=P)
+            for half in range(2):
+                rows = slice(half * NW // 2, (half + 1) * NW // 2)
+                nc.sync.dma_start(out=w_nat[:, rows, :], in_=w_rows[:, rows, :])
+            for s in range(S):
+                nc.sync.dma_start(out=x_nat[s][:], in_=x_grp[s].rearrange("(t p) k -> p t k", p=P))
+            nc.sync.dma_start(out=bias[:], in_=bv.partition_broadcast(P))
+
+            ident_bf = inputs.tile([P, P], BF16)
+            make_identity(nc, ident_bf[:])
+            ident_f32 = inputs.tile([P, P], F32)
+            make_identity(nc, ident_f32[:])
+            one = inputs.tile([P, 1], F32)
+            nc.vector.memset(one[:], 1.0)
+            nc.scalar.activation(out=one[:], in_=one[:], func=ACT.Ln)
+            q_feat = [inputs.tile([P, NT, P], BF16, name="q_feat%d" % s) for s in range(S)]
+            k_feat = [inputs.tile([P, NT, P], BF16, name="k_feat%d" % s) for s in range(S)]
+
+            def by_head(feat):
+                return feat[:, :, 0 : H * EXTRA].rearrange("p i (h j) -> p i h j", j=EXTRA)
+
+            for s in range(S):
+                nc.vector.memset(q_feat[s][:], 0.0)
+                nc.vector.memset(by_head(q_feat[s])[:, :, :, PIECES:EXTRA], 1.0)
+                nc.vector.memset(k_feat[s][:], 0.0)
+                nc.vector.memset(by_head(k_feat[s])[:, :, :, 0:PIECES], 1.0)
+            for n in range(HEADS):
+                nc.vector.memset(w_bf[n][:, 0 : NT - 1].rearrange("p i b t -> p (i b t)").bitcast(F32), 0.0)
+            head_rows = inputs.tile([P, H], F32)
+            nc.vector.tensor_reduce(
+                out=head_rows[:],
+                in_=ident_f32[:, 0 : H * EXTRA].rearrange("p (h j) -> p h j", j=EXTRA),
+                axis=AX.X,
+                op=ALU.add,
+            )
+
+            qT = inputs.tile([P, S, H, B], BF16)
+            kT = inputs.tile([P, S, H, B], BF16)
+            q_extra = inputs.tile([P, S, B], BF16)
+            k_extra = inputs.tile([P, S, H, B], BF16)
+            square = inputs.tile([P, DPP], BF16)
+
+            def sums_of_squares(nat, name):
+                sums = inputs.tile([P, H * NT], F32, name=name)
+                for h in range(H):
+                    for i in range(NT):
+                        n = h * NT + i
+                        nc.scalar.activation(
+                            out=square[:], in_=nat[:, h, i, :], func=ACT.Square, accum_out=sums[:, n : n + 1]
+                        )
+                return sums
+
+            def transposed(blocks):
+                tp = psum_t.tile([P, NT, P], BF16, tag="tp")
+                for i in range(NT):
+                    nc.tensor.transpose(tp[:, i, :], blocks[:, i, :], ident_bf[:])
+                return tp[:].rearrange("p i b -> p (i b)")
+
+            def transpose_queries(s):
+                for h in range(H):
+                    nc.vector.tensor_scalar(
+                        out=qT[:, s, h, :], in0=transposed(q_nat[s][:, h]), scalar1=-2.0, scalar2=None, op0=ALU.mult
+                    )
+
+            def transpose_keys(s):
+                for h in range(H):
+                    nc.vector.tensor_copy(out=kT[:, s, h, :], in_=transposed(k_nat[s][:, h]))
+
+            def split_in_pieces(sums, feat, first):
+                rest = sums[:].rearrange("p (h i) -> p i h", i=NT)
+                for j in range(PIECES):
+                    piece = by_head(feat)[:, :, :, first + j]
+                    nc.vector.tensor_copy(out=piece, in_=rest)
+                    if j < PIECES - 1:
+                        left = small.tile([P, NT, H], F32, tag="left")
+                        nc.vector.tensor_tensor(out=left[:], in0=rest, in1=piece, op=ALU.subtract)
+                        rest = left[:]
+
+            def transpose_extra_features(s):
+                nc.vector.tensor_copy(out=q_extra[:, s, :], in_=transposed(q_feat[s]))
+                k_rows = transposed(k_feat[s])
+                for h in range(H):
+                    nc.vector.tensor_scalar(
+                        out=k_extra[:, s, h, :], in0=k_rows, scalar1=head_rows[:, h : h + 1], scalar2=None, op0=ALU.mult
+                    )
+
+            def row_tile(n):
+                if n < NW:
+                    return w_nat[:, n, :]
+                return x_nat[(n - NW) // NT][:, (n - NW) % NT, :]
+
+            def transpose_rows(pair):
+                grouped = stage.tile([P, 2 * PASSES * P * PACK], BF16, tag="grouped", align_bytes=64)
+                words = grouped[:].bitcast(F32).rearrange("p (n g r u) -> p n g r u", n=2, g=PASSES, u=2)
+                for n in range(2):
+                    source = row_tile(2 * pair + n).bitcast(F32)
+                    tp = psum_t.tile([P, PASSES, 2, P], F32, tag="tp")
+                    for g in range(PASSES):
+                        for u in range(2):
+                            first = (2 * g + u) * P
+                            nc.tensor.transpose(tp[:, g, u, :], source[:, first : first + P], ident_f32[:])
+                    nc.scalar.copy(out=words[:, n], in_=tp[:].rearrange("p g u r -> p g r u"))
+                return grouped
+
+            def quantise_rows(pair, grouped):
+                tiles = slice(2 * pair, 2 * pair + 2)
+                nc.vector.quantize_mx(
+                    out=xw_codes[:, tiles].rearrange("p n g r -> p (n g r)").bitcast(FP8X4),
+                    scales=xw_scales[:, tiles].rearrange("p n g r -> p (n g r)"),
+                    in_=grouped[:],
+                )
+
+            def distances(s, h):
+                logd = logs.tile([P, first_column(NT)], F32, tag="logd")
+                for i in range(NT):
+                    d2 = psum_d.tile([P, NT, P], F32, tag="d2")
+                    b_cols = slice(i * P, (i + 1) * P)
+                    for t in range(i + 1):
+                        c_cols = slice(t * P, (t + 1) * P)
+                        nc.tensor.matmul(
+                            out=d2[:, t, :], lhsT=kT[:, s, h, c_cols], rhs=qT[:, s, h, b_cols], start=True, stop=False
+                        )
+                        nc.tensor.matmul(
+                            out=d2[:, t, :],
+                            lhsT=k_extra[:, s, h, c_cols],
+                            rhs=q_extra[:, s, b_cols],
+                            start=False,
+                            stop=True,
+                        )
+                    nc.vector.tensor_scalar(
+                        out=query_tile(logd, i),
+                        in0=d2[:, 0 : i + 1, :],
+                        scalar1=D2_FLOOR,
+                        scalar2=D2_CEIL,
+                        op0=ALU.max,
+                        op1=ALU.min,
+                    )
+                return logd
+
+            def logarithms(logd):
+                nc.scalar.activation(out=logd[:], in_=logd[:], func=ACT.Ln)
+                for i in range(NT):
+                    diagonal = query_tile(logd, i)[:, i, :]
+                    nc.gpsimd.affine_select(
+                        out=diagonal,
+                        in_=diagonal,
+                        pattern=[[1, P]],
+                        compare_op=ALU.is_ge,
+                        fill=MASKED_LOG,
+                        base=0,
+                        channel_multiplier=-1,
+                    )
+
+            q_sums = [sums_of_squares(q_nat[0], "q_sums0")]
+            k_sums = [sums_of_squares(k_nat[0], "k_sums0")]
+            q_sums.append(sums_of_squares(q_nat[1], "q_sums1"))
+            k_sums.append(sums_of_squares(k_nat[1], "k_sums1"))
+
+            def split_sums(s):
+                split_in_pieces(q_sums[s], q_feat[s], 0)
+                split_in_pieces(k_sums[s], k_feat[s], PIECES)
+
+            transpose_queries(0)
+            transpose_keys(0)
+            transpose_queries(1)
+            split_sums(0)
+            transpose_keys(1)
+            transpose_extra_features(0)
+
+            row_pairs = []
+            for n in range(HEADS):
+                row_pairs.append(transpose_rows(n))
+                head_logs.append(distances(n // H, n % H))
+                if n == 0:
+                    split_sums(1)
+                if n == 1:
+                    transpose_extra_features(1)
+                logarithms(head_logs[n])
+                if n > 0:
+                    quantise_rows(n - 1, row_pairs[n - 1])
+            quantise_rows(HEADS - 1, row_pairs[HEADS - 1])
+
+        with tc.tile_pool(name="outputs", bufs=HEADS) as outputs:
+
+            def weights(n):
+                for i in range(NT):
+                    nc.scalar.activation(
+                        out=w_bf[n][:, i, :, 0 : i + 1],
+                        in_=query_tile(head_logs[n], i).rearrange("p t b -> p b t"),
+                        func=ACT.Sigmoid,
+                        scale=-0.5,
+                    )
+
+            def project_values(s, part):
+                v_bf = stage.tile([P, CHUNKS, P, PACK], BF16, tag="v_bf", bufs=2, align_bytes=64)
+                for n in range(CHUNKS):
+                    j = part * CHUNKS + n
+                    v_ps = psum_m.tile([P, NT, P], F32, tag="mx")
+                    for t in range(NT):
+                        for g in range(PASSES):
+                            nc.tensor.matmul_mx(
+                                out=v_ps[:, t, :],
+                                lhsT=xw_codes[:, NW + NT * s + t, g, :].bitcast(FP8X4),
+                                lhsT_scale=xw_scales[:, NW + NT * s + t, g, :],
+                                rhs=xw_codes[:, j, g, :].bitcast(FP8X4),
+                                rhs_scale=xw_scales[:, j, g, :],
+                                start=(g == 0),
+                                stop=(g == PASSES - 1),
+                            )
+                    nc.vector.tensor_tensor(
+                        out=v_bf[:, n],
+                        in0=v_ps[:].rearrange("p t d -> p d t"),
+                        in1=bias[:, j * P : (j + 1) * P].unsqueeze(2).to_broadcast([P, P, PACK]),
+                        op=ALU.add,
+                    )
+                cols = slice(part * CHUNKS * P, (part + 1) * CHUNKS * P)
+                nc.vector.quantize_mx(
+                    out=v_codes[:, s, cols].bitcast(FP8X4),
+                    scales=v_scales[:, s, cols],
+                    in_=v_bf[:].rearrange("p n d t -> p (n d t)"),
+                )
+
+            def multiply(n):
+                s, h = n // H, n % H
+                w_codes = stage.tile([P, NT * P], U32, tag="w_codes", align_bytes=64)
+                w_scales = stage.tile([P, NT * P], U8, tag="w_scales", align_bytes=64)
+                nc.vector.quantize_mx(
+                    out=w_codes[:].bitcast(FP8X4), scales=w_scales[:], in_=w_bf[n][:].rearrange("p i b t -> p (i b t)")
+                )
+                d_cols = slice(h * DPH, (h + 1) * DPH)
+                banks = []
+                for pair in range(NT // 2):
+                    if n % 2 == 0:
+                        o_ps = psum_d.tile([P, 2, DPH], F32, tag="d2")
+                    else:
+                        o_ps = psum_m.tile([P, 2, DPH], F32, tag="mx")
+                    for e in range(2):
+                        b_cols = slice((2 * pair + e) * P, (2 * pair + e + 1) * P)
+                        nc.tensor.matmul_mx(
+                            out=o_ps[:, e, :],
+                            lhsT=w_codes[:, b_cols].bitcast(FP8X4),
+                            lhsT_scale=w_scales[:, b_cols],
+                            rhs=v_codes[:, s, d_cols].bitcast(FP8X4),
+                            rhs_scale=v_scales[:, s, d_cols],
+                            start=True,
+                            stop=True,
+                        )
+                    banks.append(o_ps)
+                return banks
+
+            def store(n, banks):
+                s, h = n // H, n % H
+                o_sb = outputs.tile([P, NT, DPH], F32, tag="o_sb")
+                nc.scalar.copy(out=o_sb[:, 0:2, :], in_=banks[0][:])
+                nc.vector.tensor_copy(out=o_sb[:, 2:4, :], in_=banks[1][:])
+                d_cols = slice(h * DPH, (h + 1) * DPH)
+                nc.sync.dma_start(out=out[s].rearrange("(i p) d -> p i d", p=P)[:, :, d_cols], in_=o_sb[:])
+
+            for n in range(HEADS):
+                weights(n)
+            for s in range(S):
+                for part in range(NW // CHUNKS):
+                    project_values(s, part)
+            head_banks = []
+            for n in range(HEADS + 1):
+                if n < HEADS:
+                    head_banks.append(multiply(n))
+                if n > 0:
+                    store(n - 1, head_banks[n - 1])

@@ -25,6 +25,7 @@ HEADS = S * H
 CHUNKS = 4
 PIECES = 3
 EXTRA = 2 * PIECES
+VECTOR_HEADS = 3
 D2_FLOOR = 1e-12
 D2_CEIL = 2.0**64
 MASKED_LOG = 1e30
@@ -46,9 +47,6 @@ def tile_networklayer_pb_kernel(tc, q_pos, k_pos, x_grp, Wv, bv, out):
         keep = ctx.enter_context(tc.tile_pool(name="keep", bufs=1))
         logs = ctx.enter_context(tc.tile_pool(name="logs", bufs=HEADS))
         stage = ctx.enter_context(tc.tile_pool(name="stage", bufs=3))
-        psum_t = ctx.enter_context(tc.psum_pool(name="psum_t", bufs=2))
-        psum_d = ctx.enter_context(tc.psum_pool(name="psum_d", bufs=3))
-        psum_m = ctx.enter_context(tc.psum_pool(name="psum_m", bufs=3))
         ctx.enter_context(tc.manual_schedule())
 
         bias = keep.tile([P, D], BF16)
@@ -59,7 +57,11 @@ def tile_networklayer_pb_kernel(tc, q_pos, k_pos, x_grp, Wv, bv, out):
         w_bf = [keep.tile([P, NT, P, PACK], BF16, name="w_bf%d" % n, align_bytes=64) for n in range(HEADS)]
         head_logs = []
 
-        with tc.tile_pool(name="inputs", bufs=1) as inputs, tc.tile_pool(name="small", bufs=2) as small:
+        with ExitStack() as first:
+            inputs = first.enter_context(tc.tile_pool(name="inputs", bufs=1))
+            small = first.enter_context(tc.tile_pool(name="small", bufs=2))
+            psum_t = first.enter_context(tc.psum_pool(name="psum_t", bufs=4))
+            psum_d = first.enter_context(tc.psum_pool(name="psum_d", bufs=4))
             q_nat = [inputs.tile([P, H, NT, DPP], BF16, name="q_nat%d" % s) for s in range(S)]
             k_nat = [inputs.tile([P, H, NT, DPP], BF16, name="k_nat%d" % s) for s in range(S)]
             w_nat = inputs.tile([P, NW, D], BF16)
@@ -90,9 +92,9 @@ def tile_networklayer_pb_kernel(tc, q_pos, k_pos, x_grp, Wv, bv, out):
 
             for s in range(S):
                 nc.vector.memset(q_feat[s][:], 0.0)
-                nc.vector.memset(by_head(q_feat[s])[:, :, :, PIECES:EXTRA], 1.0)
+                nc.vector.memset(by_head(q_feat[s])[:, :, :, PIECES:EXTRA], -0.5)
                 nc.vector.memset(k_feat[s][:], 0.0)
-                nc.vector.memset(by_head(k_feat[s])[:, :, :, 0:PIECES], 1.0)
+                nc.vector.memset(by_head(k_feat[s])[:, :, :, 0:PIECES], -0.5)
             for n in range(HEADS):
                 nc.vector.memset(w_bf[n][:, 0 : NT - 1].rearrange("p i b t -> p (i b t)").bitcast(F32), 0.0)
             head_rows = inputs.tile([P, H], F32)
@@ -127,9 +129,7 @@ def tile_networklayer_pb_kernel(tc, q_pos, k_pos, x_grp, Wv, bv, out):
 
             def transpose_queries(s):
                 for h in range(H):
-                    nc.vector.tensor_scalar(
-                        out=qT[:, s, h, :], in0=transposed(q_nat[s][:, h]), scalar1=-2.0, scalar2=None, op0=ALU.mult
-                    )
+                    nc.vector.tensor_copy(out=qT[:, s, h, :], in_=transposed(q_nat[s][:, h]))
 
             def transpose_keys(s):
                 for h in range(H):
@@ -182,15 +182,15 @@ def tile_networklayer_pb_kernel(tc, q_pos, k_pos, x_grp, Wv, bv, out):
             def distances(s, h):
                 logd = logs.tile([P, first_column(NT)], F32, tag="logd")
                 for i in range(NT):
-                    d2 = psum_d.tile([P, NT, P], F32, tag="d2")
+                    dots = psum_d.tile([P, NT, P], F32, tag="dots")
                     b_cols = slice(i * P, (i + 1) * P)
                     for t in range(i + 1):
                         c_cols = slice(t * P, (t + 1) * P)
                         nc.tensor.matmul(
-                            out=d2[:, t, :], lhsT=kT[:, s, h, c_cols], rhs=qT[:, s, h, b_cols], start=True, stop=False
+                            out=dots[:, t, :], lhsT=kT[:, s, h, c_cols], rhs=qT[:, s, h, b_cols], start=True, stop=False
                         )
                         nc.tensor.matmul(
-                            out=d2[:, t, :],
+                            out=dots[:, t, :],
                             lhsT=k_extra[:, s, h, c_cols],
                             rhs=q_extra[:, s, b_cols],
                             start=False,
@@ -198,16 +198,16 @@ def tile_networklayer_pb_kernel(tc, q_pos, k_pos, x_grp, Wv, bv, out):
                         )
                     nc.vector.tensor_scalar(
                         out=query_tile(logd, i),
-                        in0=d2[:, 0 : i + 1, :],
-                        scalar1=D2_FLOOR,
-                        scalar2=D2_CEIL,
-                        op0=ALU.max,
-                        op1=ALU.min,
+                        in0=dots[:, 0 : i + 1, :],
+                        scalar1=-0.5 * D2_FLOOR,
+                        scalar2=-0.5 * D2_CEIL,
+                        op0=ALU.min,
+                        op1=ALU.max,
                     )
                 return logd
 
             def logarithms(logd):
-                nc.scalar.activation(out=logd[:], in_=logd[:], func=ACT.Ln)
+                nc.scalar.activation(out=logd[:], in_=logd[:], func=ACT.Ln, scale=-2.0)
                 for i in range(NT):
                     diagonal = query_tile(logd, i)[:, i, :]
                     nc.gpsimd.affine_select(
@@ -249,7 +249,10 @@ def tile_networklayer_pb_kernel(tc, q_pos, k_pos, x_grp, Wv, bv, out):
                     quantise_rows(n - 1, row_pairs[n - 1])
             quantise_rows(HEADS - 1, row_pairs[HEADS - 1])
 
-        with tc.tile_pool(name="outputs", bufs=HEADS) as outputs:
+        with ExitStack() as second:
+            outputs = second.enter_context(tc.tile_pool(name="outputs", bufs=HEADS))
+            psum_v = second.enter_context(tc.psum_pool(name="psum_v", bufs=4))
+            psum_o = second.enter_context(tc.psum_pool(name="psum_o", bufs=4))
 
             def weights(n):
                 for i in range(NT):
@@ -264,7 +267,7 @@ def tile_networklayer_pb_kernel(tc, q_pos, k_pos, x_grp, Wv, bv, out):
                 v_bf = stage.tile([P, CHUNKS, P, PACK], BF16, tag="v_bf", bufs=2, align_bytes=64)
                 for n in range(CHUNKS):
                     j = part * CHUNKS + n
-                    v_ps = psum_m.tile([P, NT, P], F32, tag="mx")
+                    v_ps = psum_v.tile([P, NT, P], F32, tag="v_ps")
                     for t in range(NT):
                         for g in range(PASSES):
                             nc.tensor.matmul_mx(
@@ -299,10 +302,7 @@ def tile_networklayer_pb_kernel(tc, q_pos, k_pos, x_grp, Wv, bv, out):
                 d_cols = slice(h * DPH, (h + 1) * DPH)
                 banks = []
                 for pair in range(NT // 2):
-                    if n % 2 == 0:
-                        o_ps = psum_d.tile([P, 2, DPH], F32, tag="d2")
-                    else:
-                        o_ps = psum_m.tile([P, 2, DPH], F32, tag="mx")
+                    o_ps = psum_o.tile([P, 2, DPH], F32, tag="o_ps")
                     for e in range(2):
                         b_cols = slice((2 * pair + e) * P, (2 * pair + e + 1) * P)
                         nc.tensor.matmul_mx(
@@ -320,7 +320,10 @@ def tile_networklayer_pb_kernel(tc, q_pos, k_pos, x_grp, Wv, bv, out):
             def store(n, banks):
                 s, h = n // H, n % H
                 o_sb = outputs.tile([P, NT, DPH], F32, tag="o_sb")
-                nc.scalar.copy(out=o_sb[:, 0:2, :], in_=banks[0][:])
+                if n < VECTOR_HEADS:
+                    nc.vector.tensor_copy(out=o_sb[:, 0:2, :], in_=banks[0][:])
+                else:
+                    nc.scalar.copy(out=o_sb[:, 0:2, :], in_=banks[0][:])
                 nc.vector.tensor_copy(out=o_sb[:, 2:4, :], in_=banks[1][:])
                 d_cols = slice(h * DPH, (h + 1) * DPH)
                 nc.sync.dma_start(out=out[s].rearrange("(i p) d -> p i d", p=P)[:, :, d_cols], in_=o_sb[:])

@@ -23,9 +23,10 @@ PASSES = D // (P * PACK)
 NW = D // P
 HEADS = S * H
 CHUNKS = 4
+BANK_BLOCKS = 4
 PIECES = 3
 EXTRA = 2 * PIECES
-VECTOR_HEADS = 3
+VECTOR_HEADS = 4
 D2_FLOOR = 1e-12
 D2_CEIL = 2.0**64
 MASKED_LOG = 1e30
@@ -96,7 +97,7 @@ def tile_networklayer_pb_kernel(tc, q_pos, k_pos, x_grp, Wv, bv, out):
                 nc.vector.memset(k_feat[s][:], 0.0)
                 nc.vector.memset(by_head(k_feat[s])[:, :, :, 0:PIECES], -0.5)
             for n in range(HEADS):
-                nc.vector.memset(w_bf[n][:, 0 : NT - 1].rearrange("p i b t -> p (i b t)").bitcast(F32), 0.0)
+                nc.gpsimd.memset(w_bf[n][:, 0 : NT - 1].rearrange("p i b t -> p (i b t)").bitcast(F32), 0.0)
             head_rows = inputs.tile([P, H], F32)
             nc.vector.tensor_reduce(
                 out=head_rows[:],
@@ -105,8 +106,7 @@ def tile_networklayer_pb_kernel(tc, q_pos, k_pos, x_grp, Wv, bv, out):
                 op=ALU.add,
             )
 
-            qT = inputs.tile([P, S, H, B], BF16)
-            kT = inputs.tile([P, S, H, B], BF16)
+            qkT = inputs.tile([P, S, H, 2, B], BF16)
             q_extra = inputs.tile([P, S, B], BF16)
             k_extra = inputs.tile([P, S, H, B], BF16)
             square = inputs.tile([P, DPP], BF16)
@@ -127,13 +127,14 @@ def tile_networklayer_pb_kernel(tc, q_pos, k_pos, x_grp, Wv, bv, out):
                     nc.tensor.transpose(tp[:, i, :], blocks[:, i, :], ident_bf[:])
                 return tp[:].rearrange("p i b -> p (i b)")
 
-            def transpose_queries(s):
+            def transpose_positions(s):
                 for h in range(H):
-                    nc.vector.tensor_copy(out=qT[:, s, h, :], in_=transposed(q_nat[s][:, h]))
-
-            def transpose_keys(s):
-                for h in range(H):
-                    nc.vector.tensor_copy(out=kT[:, s, h, :], in_=transposed(k_nat[s][:, h]))
+                    tp = psum_t.tile([P, 2, NT, P], BF16, tag="tp")
+                    for i in range(NT):
+                        nc.tensor.transpose(tp[:, 0, i, :], q_nat[s][:, h, i, :], ident_bf[:])
+                    for i in range(NT):
+                        nc.tensor.transpose(tp[:, 1, i, :], k_nat[s][:, h, i, :], ident_bf[:])
+                    nc.vector.tensor_copy(out=qkT[:, s, h], in_=tp[:].rearrange("p x i b -> p x (i b)"))
 
             def split_in_pieces(sums, feat, first):
                 rest = sums[:].rearrange("p (h i) -> p i h", i=NT)
@@ -181,24 +182,30 @@ def tile_networklayer_pb_kernel(tc, q_pos, k_pos, x_grp, Wv, bv, out):
 
             def distances(s, h):
                 logd = logs.tile([P, first_column(NT)], F32, tag="logd")
-                for i in range(NT):
-                    dots = psum_d.tile([P, NT, P], F32, tag="dots")
-                    b_cols = slice(i * P, (i + 1) * P)
-                    for t in range(i + 1):
+                blocks = [(i, t) for i in range(NT) for t in range(i + 1)]
+                for first in range(0, len(blocks), BANK_BLOCKS):
+                    in_bank = blocks[first : first + BANK_BLOCKS]
+                    dots = psum_d.tile([P, BANK_BLOCKS, P], F32, tag="dots")
+                    for m, (i, t) in enumerate(in_bank):
+                        b_cols = slice(i * P, (i + 1) * P)
                         c_cols = slice(t * P, (t + 1) * P)
                         nc.tensor.matmul(
-                            out=dots[:, t, :], lhsT=kT[:, s, h, c_cols], rhs=qT[:, s, h, b_cols], start=True, stop=False
+                            out=dots[:, m, :],
+                            lhsT=qkT[:, s, h, 1, c_cols],
+                            rhs=qkT[:, s, h, 0, b_cols],
+                            start=True,
+                            stop=False,
                         )
                         nc.tensor.matmul(
-                            out=dots[:, t, :],
+                            out=dots[:, m, :],
                             lhsT=k_extra[:, s, h, c_cols],
                             rhs=q_extra[:, s, b_cols],
                             start=False,
                             stop=True,
                         )
                     nc.vector.tensor_scalar(
-                        out=query_tile(logd, i),
-                        in0=dots[:, 0 : i + 1, :],
+                        out=logd[:, first * P : (first + len(in_bank)) * P],
+                        in0=dots[:, 0 : len(in_bank), :].rearrange("p m b -> p (m b)"),
                         scalar1=-0.5 * D2_FLOOR,
                         scalar2=-0.5 * D2_CEIL,
                         op0=ALU.min,
@@ -229,11 +236,9 @@ def tile_networklayer_pb_kernel(tc, q_pos, k_pos, x_grp, Wv, bv, out):
                 split_in_pieces(q_sums[s], q_feat[s], 0)
                 split_in_pieces(k_sums[s], k_feat[s], PIECES)
 
-            transpose_queries(0)
-            transpose_keys(0)
-            transpose_queries(1)
+            transpose_positions(0)
             split_sums(0)
-            transpose_keys(1)
+            transpose_positions(1)
             transpose_extra_features(0)
 
             row_pairs = []
@@ -320,11 +325,11 @@ def tile_networklayer_pb_kernel(tc, q_pos, k_pos, x_grp, Wv, bv, out):
             def store(n, banks):
                 s, h = n // H, n % H
                 o_sb = outputs.tile([P, NT, DPH], F32, tag="o_sb")
-                if n < VECTOR_HEADS:
-                    nc.vector.tensor_copy(out=o_sb[:, 0:2, :], in_=banks[0][:])
-                else:
-                    nc.scalar.copy(out=o_sb[:, 0:2, :], in_=banks[0][:])
-                nc.vector.tensor_copy(out=o_sb[:, 2:4, :], in_=banks[1][:])
+                for pair in range(NT // 2):
+                    if n < VECTOR_HEADS:
+                        nc.vector.tensor_copy(out=o_sb[:, 2 * pair : 2 * pair + 2, :], in_=banks[pair][:])
+                    else:
+                        nc.scalar.copy(out=o_sb[:, 2 * pair : 2 * pair + 2, :], in_=banks[pair][:])
                 d_cols = slice(h * DPH, (h + 1) * DPH)
                 nc.sync.dma_start(out=out[s].rearrange("(i p) d -> p i d", p=P)[:, :, d_cols], in_=o_sb[:])
 

@@ -22,11 +22,9 @@ NT = B // P
 PASSES = D // (P * PACK)
 NW = D // P
 HEADS = S * H
-CHUNKS = 4
 BANK_BLOCKS = 4
 PIECES = 3
 EXTRA = 2 * PIECES
-VECTOR_HEADS = 4
 D2_FLOOR = 1e-12
 D2_CEIL = 2.0**64
 MASKED_LOG = 1e30
@@ -46,8 +44,7 @@ def tile_networklayer_pb_kernel(tc, q_pos, k_pos, x_grp, Wv, bv, out):
     nc = tc.nc
     with ExitStack() as ctx:
         keep = ctx.enter_context(tc.tile_pool(name="keep", bufs=1))
-        logs = ctx.enter_context(tc.tile_pool(name="logs", bufs=HEADS))
-        stage = ctx.enter_context(tc.tile_pool(name="stage", bufs=3))
+        logs = ctx.enter_context(tc.tile_pool(name="logs", bufs=S))
         ctx.enter_context(tc.manual_schedule())
 
         bias = keep.tile([P, D], BF16)
@@ -55,25 +52,30 @@ def tile_networklayer_pb_kernel(tc, q_pos, k_pos, x_grp, Wv, bv, out):
         xw_scales = keep.tile([P, NW + S * NT, PASSES, P], U8, align_bytes=64)
         v_codes = keep.tile([P, S, D], U32, align_bytes=64)
         v_scales = keep.tile([P, S, D], U8, align_bytes=64)
-        w_bf = [keep.tile([P, NT, P, PACK], BF16, name="w_bf%d" % n, align_bytes=64) for n in range(HEADS)]
-        head_logs = []
+        w_bf = [keep.tile([P, H, NT, P, PACK], BF16, name="w_bf%d" % s, align_bytes=64) for s in range(S)]
+        group_logs = [logs.tile([P, H, first_column(NT)], F32, name="group_logs%d" % s, tag="group_logs") for s in range(S)]
 
-        with ExitStack() as first:
-            inputs = first.enter_context(tc.tile_pool(name="inputs", bufs=1))
-            small = first.enter_context(tc.tile_pool(name="small", bufs=2))
-            psum_t = first.enter_context(tc.psum_pool(name="psum_t", bufs=4))
-            psum_d = first.enter_context(tc.psum_pool(name="psum_d", bufs=4))
+        with ExitStack() as part_one:
+            inputs = part_one.enter_context(tc.tile_pool(name="inputs", bufs=1))
+            small = part_one.enter_context(tc.tile_pool(name="small", bufs=2))
+            stage = part_one.enter_context(tc.tile_pool(name="stage", bufs=3))
+            psum_t = part_one.enter_context(tc.psum_pool(name="psum_t", bufs=4))
+            psum_d = part_one.enter_context(tc.psum_pool(name="psum_d", bufs=4))
             q_nat = [inputs.tile([P, H, NT, DPP], BF16, name="q_nat%d" % s) for s in range(S)]
             k_nat = [inputs.tile([P, H, NT, DPP], BF16, name="k_nat%d" % s) for s in range(S)]
             w_nat = inputs.tile([P, NW, D], BF16)
             x_nat = [inputs.tile([P, NT, D], BF16, name="x_nat%d" % s) for s in range(S)]
-            for s in range(S):
+
+            def load_positions(s):
                 nc.sync.dma_start(out=q_nat[s][:], in_=q_pos[s].rearrange("h (i p) f -> p h i f", p=P))
                 nc.sync.dma_start(out=k_nat[s][:], in_=k_pos[s].rearrange("h (i p) f -> p h i f", p=P))
+
+            load_positions(0)
             w_rows = Wv.rearrange("(j p) k -> p j k", p=P)
             for half in range(2):
                 rows = slice(half * NW // 2, (half + 1) * NW // 2)
                 nc.sync.dma_start(out=w_nat[:, rows, :], in_=w_rows[:, rows, :])
+            load_positions(1)
             for s in range(S):
                 nc.sync.dma_start(out=x_nat[s][:], in_=x_grp[s].rearrange("(t p) k -> p t k", p=P))
             nc.sync.dma_start(out=bias[:], in_=bv.partition_broadcast(P))
@@ -96,8 +98,9 @@ def tile_networklayer_pb_kernel(tc, q_pos, k_pos, x_grp, Wv, bv, out):
                 nc.vector.memset(by_head(q_feat[s])[:, :, :, PIECES:EXTRA], -0.5)
                 nc.vector.memset(k_feat[s][:], 0.0)
                 nc.vector.memset(by_head(k_feat[s])[:, :, :, 0:PIECES], -0.5)
-            for n in range(HEADS):
-                nc.gpsimd.memset(w_bf[n][:, 0 : NT - 1].rearrange("p i b t -> p (i b t)").bitcast(F32), 0.0)
+            for s in range(S):
+                for h in range(H):
+                    nc.gpsimd.memset(w_bf[s][:, h, 0 : NT - 1].rearrange("p i b t -> p (i b t)").bitcast(F32), 0.0)
             head_rows = inputs.tile([P, H], F32)
             nc.vector.tensor_reduce(
                 out=head_rows[:],
@@ -109,17 +112,19 @@ def tile_networklayer_pb_kernel(tc, q_pos, k_pos, x_grp, Wv, bv, out):
             qkT = inputs.tile([P, S, H, 2, B], BF16)
             q_extra = inputs.tile([P, S, B], BF16)
             k_extra = inputs.tile([P, S, H, B], BF16)
-            square = inputs.tile([P, DPP], BF16)
 
             def sums_of_squares(nat, name):
+                squares = small.tile([P, H * NT, DPP], F32, tag="squares")
+                nc.scalar.activation(out=squares[:], in_=nat[:].rearrange("p h i f -> p (h i) f"), func=ACT.Square)
                 sums = inputs.tile([P, H * NT], F32, name=name)
-                for h in range(H):
-                    for i in range(NT):
-                        n = h * NT + i
-                        nc.scalar.activation(
-                            out=square[:], in_=nat[:, h, i, :], func=ACT.Square, accum_out=sums[:, n : n + 1]
-                        )
+                nc.vector.tensor_reduce(out=sums[:], in_=squares[:], axis=AX.X, op=ALU.add)
                 return sums
+
+            def extra_features(s):
+                q_sums = sums_of_squares(q_nat[s], "q_sums%d" % s)
+                k_sums = sums_of_squares(k_nat[s], "k_sums%d" % s)
+                split_in_pieces(q_sums, q_feat[s], 0)
+                split_in_pieces(k_sums, k_feat[s], PIECES)
 
             def transposed(blocks):
                 tp = psum_t.tile([P, NT, P], BF16, tag="tp")
@@ -134,7 +139,7 @@ def tile_networklayer_pb_kernel(tc, q_pos, k_pos, x_grp, Wv, bv, out):
                         nc.tensor.transpose(tp[:, 0, i, :], q_nat[s][:, h, i, :], ident_bf[:])
                     for i in range(NT):
                         nc.tensor.transpose(tp[:, 1, i, :], k_nat[s][:, h, i, :], ident_bf[:])
-                    nc.vector.tensor_copy(out=qkT[:, s, h], in_=tp[:].rearrange("p x i b -> p x (i b)"))
+                    nc.scalar.copy(out=qkT[:, s, h], in_=tp[:].rearrange("p x i b -> p x (i b)"))
 
             def split_in_pieces(sums, feat, first):
                 rest = sums[:].rearrange("p (h i) -> p i h", i=NT)
@@ -181,7 +186,7 @@ def tile_networklayer_pb_kernel(tc, q_pos, k_pos, x_grp, Wv, bv, out):
                 )
 
             def distances(s, h):
-                logd = logs.tile([P, first_column(NT)], F32, tag="logd")
+                logd = group_logs[s][:, h, :]
                 blocks = [(i, t) for i in range(NT) for t in range(i + 1)]
                 for first in range(0, len(blocks), BANK_BLOCKS):
                     in_bank = blocks[first : first + BANK_BLOCKS]
@@ -214,7 +219,7 @@ def tile_networklayer_pb_kernel(tc, q_pos, k_pos, x_grp, Wv, bv, out):
                 return logd
 
             def logarithms(logd):
-                nc.scalar.activation(out=logd[:], in_=logd[:], func=ACT.Ln, scale=-2.0)
+                nc.scalar.activation(out=logd, in_=logd, func=ACT.Ln, scale=-2.0)
                 for i in range(NT):
                     diagonal = query_tile(logd, i)[:, i, :]
                     nc.gpsimd.affine_select(
@@ -227,51 +232,45 @@ def tile_networklayer_pb_kernel(tc, q_pos, k_pos, x_grp, Wv, bv, out):
                         channel_multiplier=-1,
                     )
 
-            q_sums = [sums_of_squares(q_nat[0], "q_sums0")]
-            k_sums = [sums_of_squares(k_nat[0], "k_sums0")]
-            q_sums.append(sums_of_squares(q_nat[1], "q_sums1"))
-            k_sums.append(sums_of_squares(k_nat[1], "k_sums1"))
-
-            def split_sums(s):
-                split_in_pieces(q_sums[s], q_feat[s], 0)
-                split_in_pieces(k_sums[s], k_feat[s], PIECES)
-
+            extra_features(0)
             transpose_positions(0)
-            split_sums(0)
-            transpose_positions(1)
             transpose_extra_features(0)
 
             row_pairs = []
             for n in range(HEADS):
                 row_pairs.append(transpose_rows(n))
-                head_logs.append(distances(n // H, n % H))
+                logd = distances(n // H, n % H)
                 if n == 0:
-                    split_sums(1)
+                    extra_features(1)
                 if n == 1:
+                    transpose_positions(1)
+                if n == 2:
                     transpose_extra_features(1)
-                logarithms(head_logs[n])
+                logarithms(logd)
                 if n > 0:
                     quantise_rows(n - 1, row_pairs[n - 1])
             quantise_rows(HEADS - 1, row_pairs[HEADS - 1])
 
-        with ExitStack() as second:
-            outputs = second.enter_context(tc.tile_pool(name="outputs", bufs=HEADS))
-            psum_v = second.enter_context(tc.psum_pool(name="psum_v", bufs=4))
-            psum_o = second.enter_context(tc.psum_pool(name="psum_o", bufs=4))
+        with ExitStack() as part_two:
+            outputs = part_two.enter_context(tc.tile_pool(name="outputs", bufs=HEADS))
+            work = part_two.enter_context(tc.tile_pool(name="work", bufs=2))
+            psum_v = part_two.enter_context(tc.psum_pool(name="psum_v", bufs=4))
+            psum_o = part_two.enter_context(tc.psum_pool(name="psum_o", bufs=4))
 
-            def weights(n):
+            def weights(s, pair):
+                heads = slice(2 * pair, 2 * pair + 2)
                 for i in range(NT):
+                    logd = group_logs[s][:, heads, first_column(i) : first_column(i + 1)]
                     nc.scalar.activation(
-                        out=w_bf[n][:, i, :, 0 : i + 1],
-                        in_=query_tile(head_logs[n], i).rearrange("p t b -> p b t"),
+                        out=w_bf[s][:, heads, i, :, 0 : i + 1],
+                        in_=logd.rearrange("p h (t b) -> p h b t", t=i + 1),
                         func=ACT.Sigmoid,
                         scale=-0.5,
                     )
 
-            def project_values(s, part):
-                v_bf = stage.tile([P, CHUNKS, P, PACK], BF16, tag="v_bf", bufs=2, align_bytes=64)
-                for n in range(CHUNKS):
-                    j = part * CHUNKS + n
+            def project_values(s):
+                v_bf = work.tile([P, NW, P, PACK], BF16, tag="v_bf", align_bytes=64)
+                for j in range(NW):
                     v_ps = psum_v.tile([P, NT, P], F32, tag="v_ps")
                     for t in range(NT):
                         for g in range(PASSES):
@@ -285,62 +284,67 @@ def tile_networklayer_pb_kernel(tc, q_pos, k_pos, x_grp, Wv, bv, out):
                                 stop=(g == PASSES - 1),
                             )
                     nc.vector.tensor_tensor(
-                        out=v_bf[:, n],
+                        out=v_bf[:, j],
                         in0=v_ps[:].rearrange("p t d -> p d t"),
                         in1=bias[:, j * P : (j + 1) * P].unsqueeze(2).to_broadcast([P, P, PACK]),
                         op=ALU.add,
                     )
-                cols = slice(part * CHUNKS * P, (part + 1) * CHUNKS * P)
                 nc.vector.quantize_mx(
-                    out=v_codes[:, s, cols].bitcast(FP8X4),
-                    scales=v_scales[:, s, cols],
-                    in_=v_bf[:].rearrange("p n d t -> p (n d t)"),
+                    out=v_codes[:, s, :].bitcast(FP8X4),
+                    scales=v_scales[:, s, :],
+                    in_=v_bf[:].rearrange("p j d t -> p (j d t)"),
                 )
 
-            def multiply(n):
-                s, h = n // H, n % H
-                w_codes = stage.tile([P, NT * P], U32, tag="w_codes", align_bytes=64)
-                w_scales = stage.tile([P, NT * P], U8, tag="w_scales", align_bytes=64)
+            def multiply(s, pair):
+                w_codes = work.tile([P, 2, NT * P], U32, tag="w_codes", align_bytes=64)
+                w_scales = work.tile([P, 2, NT * P], U8, tag="w_scales", align_bytes=64)
                 nc.vector.quantize_mx(
-                    out=w_codes[:].bitcast(FP8X4), scales=w_scales[:], in_=w_bf[n][:].rearrange("p i b t -> p (i b t)")
+                    out=w_codes[:].rearrange("p h w -> p (h w)").bitcast(FP8X4),
+                    scales=w_scales[:].rearrange("p h w -> p (h w)"),
+                    in_=w_bf[s][:, 2 * pair : 2 * pair + 2].rearrange("p h i b t -> p (h i b t)"),
                 )
-                d_cols = slice(h * DPH, (h + 1) * DPH)
                 banks = []
-                for pair in range(NT // 2):
-                    o_ps = psum_o.tile([P, 2, DPH], F32, tag="o_ps")
-                    for e in range(2):
-                        b_cols = slice((2 * pair + e) * P, (2 * pair + e + 1) * P)
-                        nc.tensor.matmul_mx(
-                            out=o_ps[:, e, :],
-                            lhsT=w_codes[:, b_cols].bitcast(FP8X4),
-                            lhsT_scale=w_scales[:, b_cols],
-                            rhs=v_codes[:, s, d_cols].bitcast(FP8X4),
-                            rhs_scale=v_scales[:, s, d_cols],
-                            start=True,
-                            stop=True,
-                        )
-                    banks.append(o_ps)
+                for e in range(2):
+                    d_cols = slice((2 * pair + e) * DPH, (2 * pair + e + 1) * DPH)
+                    for half in range(NT // 2):
+                        if pair % 2 == 0:
+                            o_ps = psum_o.tile([P, 2, DPH], F32, tag="o_ps")
+                        else:
+                            o_ps = psum_v.tile([P, 2, DPH], F32, tag="v_ps")
+                        for m in range(2):
+                            b_cols = slice((2 * half + m) * P, (2 * half + m + 1) * P)
+                            nc.tensor.matmul_mx(
+                                out=o_ps[:, m, :],
+                                lhsT=w_codes[:, e, b_cols].bitcast(FP8X4),
+                                lhsT_scale=w_scales[:, e, b_cols],
+                                rhs=v_codes[:, s, d_cols].bitcast(FP8X4),
+                                rhs_scale=v_scales[:, s, d_cols],
+                                start=True,
+                                stop=True,
+                            )
+                        banks.append(o_ps)
                 return banks
 
-            def store(n, banks):
-                s, h = n // H, n % H
-                o_sb = outputs.tile([P, NT, DPH], F32, tag="o_sb")
-                for pair in range(NT // 2):
-                    if n < VECTOR_HEADS:
-                        nc.vector.tensor_copy(out=o_sb[:, 2 * pair : 2 * pair + 2, :], in_=banks[pair][:])
-                    else:
-                        nc.scalar.copy(out=o_sb[:, 2 * pair : 2 * pair + 2, :], in_=banks[pair][:])
-                d_cols = slice(h * DPH, (h + 1) * DPH)
-                nc.sync.dma_start(out=out[s].rearrange("(i p) d -> p i d", p=P)[:, :, d_cols], in_=o_sb[:])
+            def store(s, pair, banks):
+                for e in range(2):
+                    o_sb = outputs.tile([P, NT, DPH], F32, tag="o_sb")
+                    for half in range(NT // 2):
+                        if s == 0:
+                            nc.vector.tensor_copy(out=o_sb[:, 2 * half : 2 * half + 2, :], in_=banks[2 * e + half][:])
+                        else:
+                            nc.scalar.copy(out=o_sb[:, 2 * half : 2 * half + 2, :], in_=banks[2 * e + half][:])
+                    d_cols = slice((2 * pair + e) * DPH, (2 * pair + e + 1) * DPH)
+                    nc.sync.dma_start(out=out[s].rearrange("(i p) d -> p i d", p=P)[:, :, d_cols], in_=o_sb[:])
 
-            for n in range(HEADS):
-                weights(n)
             for s in range(S):
-                for part in range(NW // CHUNKS):
-                    project_values(s, part)
-            head_banks = []
-            for n in range(HEADS + 1):
-                if n < HEADS:
-                    head_banks.append(multiply(n))
+                for pair in range(H // 2):
+                    weights(s, pair)
+            for s in range(S):
+                project_values(s)
+            PAIRS = H // 2
+            pair_banks = []
+            for n in range(S * PAIRS + 1):
+                if n < S * PAIRS:
+                    pair_banks.append(multiply(n // PAIRS, n % PAIRS))
                 if n > 0:
-                    store(n - 1, head_banks[n - 1])
+                    store((n - 1) // PAIRS, (n - 1) % PAIRS, pair_banks[n - 1])

@@ -23,6 +23,7 @@ PASSES = D // (P * PACK)
 NW = D // P
 HEADS = S * H
 BANK_BLOCKS = 4
+VECTOR_TILES = 2
 PIECES = 3
 EXTRA = 2 * PIECES
 D2_FLOOR = 1e-12
@@ -52,7 +53,7 @@ def tile_networklayer_pb_kernel(tc, q_pos, k_pos, x_grp, Wv, bv, out):
         xw_scales = keep.tile([P, NW + S * NT, PASSES, P], U8, align_bytes=64)
         v_codes = keep.tile([P, S, D], U32, align_bytes=64)
         v_scales = keep.tile([P, S, D], U8, align_bytes=64)
-        w_bf = [keep.tile([P, H, NT, P, PACK], BF16, name="w_bf%d" % s, align_bytes=64) for s in range(S)]
+        w_bf = [keep.tile([P, NT, H, P, PACK], BF16, name="w_bf%d" % s, align_bytes=64) for s in range(S)]
         group_logs = [logs.tile([P, H, first_column(NT)], F32, name="group_logs%d" % s, tag="group_logs") for s in range(S)]
 
         with ExitStack() as part_one:
@@ -99,8 +100,8 @@ def tile_networklayer_pb_kernel(tc, q_pos, k_pos, x_grp, Wv, bv, out):
                 nc.vector.memset(k_feat[s][:], 0.0)
                 nc.vector.memset(by_head(k_feat[s])[:, :, :, 0:PIECES], -0.5)
             for s in range(S):
-                for h in range(H):
-                    nc.gpsimd.memset(w_bf[s][:, h, 0 : NT - 1].rearrange("p i b t -> p (i b t)").bitcast(F32), 0.0)
+                for i in range(NT - 1):
+                    nc.gpsimd.memset(w_bf[s][:, i].rearrange("p h b t -> p (h b t)").bitcast(F32), 0.0)
             head_rows = inputs.tile([P, H], F32)
             nc.vector.tensor_reduce(
                 out=head_rows[:],
@@ -257,16 +258,14 @@ def tile_networklayer_pb_kernel(tc, q_pos, k_pos, x_grp, Wv, bv, out):
             psum_v = part_two.enter_context(tc.psum_pool(name="psum_v", bufs=4))
             psum_o = part_two.enter_context(tc.psum_pool(name="psum_o", bufs=4))
 
-            def weights(s, pair):
-                heads = slice(2 * pair, 2 * pair + 2)
-                for i in range(NT):
-                    logd = group_logs[s][:, heads, first_column(i) : first_column(i + 1)]
-                    nc.scalar.activation(
-                        out=w_bf[s][:, heads, i, :, 0 : i + 1],
-                        in_=logd.rearrange("p h (t b) -> p h b t", t=i + 1),
-                        func=ACT.Sigmoid,
-                        scale=-0.5,
-                    )
+            def weights(s, i):
+                logd = group_logs[s][:, :, first_column(i) : first_column(i + 1)]
+                nc.scalar.activation(
+                    out=w_bf[s][:, i, :, :, 0 : i + 1],
+                    in_=logd.rearrange("p h (t b) -> p h b t", t=i + 1),
+                    func=ACT.Sigmoid,
+                    scale=-0.5,
+                )
 
             def project_values(s):
                 v_bf = work.tile([P, NW, P, PACK], BF16, tag="v_bf", align_bytes=64)
@@ -295,56 +294,49 @@ def tile_networklayer_pb_kernel(tc, q_pos, k_pos, x_grp, Wv, bv, out):
                     in_=v_bf[:].rearrange("p j d t -> p (j d t)"),
                 )
 
-            def multiply(s, pair):
-                w_codes = work.tile([P, 2, NT * P], U32, tag="w_codes", align_bytes=64)
-                w_scales = work.tile([P, 2, NT * P], U8, tag="w_scales", align_bytes=64)
+            def multiply(s, i):
+                w_codes = work.tile([P, H, P], U32, tag="w_codes", align_bytes=64)
+                w_scales = work.tile([P, H, P], U8, tag="w_scales", align_bytes=64)
                 nc.vector.quantize_mx(
-                    out=w_codes[:].rearrange("p h w -> p (h w)").bitcast(FP8X4),
-                    scales=w_scales[:].rearrange("p h w -> p (h w)"),
-                    in_=w_bf[s][:, 2 * pair : 2 * pair + 2].rearrange("p h i b t -> p (h i b t)"),
+                    out=w_codes[:].rearrange("p h b -> p (h b)").bitcast(FP8X4),
+                    scales=w_scales[:].rearrange("p h b -> p (h b)"),
+                    in_=w_bf[s][:, i].rearrange("p h b t -> p (h b t)"),
                 )
                 banks = []
-                for e in range(2):
-                    d_cols = slice((2 * pair + e) * DPH, (2 * pair + e + 1) * DPH)
-                    for half in range(NT // 2):
-                        if pair % 2 == 0:
-                            o_ps = psum_o.tile([P, 2, DPH], F32, tag="o_ps")
-                        else:
-                            o_ps = psum_v.tile([P, 2, DPH], F32, tag="v_ps")
-                        for m in range(2):
-                            b_cols = slice((2 * half + m) * P, (2 * half + m + 1) * P)
-                            nc.tensor.matmul_mx(
-                                out=o_ps[:, m, :],
-                                lhsT=w_codes[:, e, b_cols].bitcast(FP8X4),
-                                lhsT_scale=w_scales[:, e, b_cols],
-                                rhs=v_codes[:, s, d_cols].bitcast(FP8X4),
-                                rhs_scale=v_scales[:, s, d_cols],
-                                start=True,
-                                stop=True,
-                            )
-                        banks.append(o_ps)
+                for pair in range(H // 2):
+                    o_ps = psum_o.tile([P, 2, DPH], F32, tag="o_ps")
+                    for e in range(2):
+                        h = 2 * pair + e
+                        d_cols = slice(h * DPH, (h + 1) * DPH)
+                        nc.tensor.matmul_mx(
+                            out=o_ps[:, e, :],
+                            lhsT=w_codes[:, h, :].bitcast(FP8X4),
+                            lhsT_scale=w_scales[:, h, :],
+                            rhs=v_codes[:, s, d_cols].bitcast(FP8X4),
+                            rhs_scale=v_scales[:, s, d_cols],
+                            start=True,
+                            stop=True,
+                        )
+                    banks.append(o_ps)
                 return banks
 
-            def store(s, pair, banks):
-                for e in range(2):
-                    o_sb = outputs.tile([P, NT, DPH], F32, tag="o_sb")
-                    for half in range(NT // 2):
-                        if s == 0:
-                            nc.vector.tensor_copy(out=o_sb[:, 2 * half : 2 * half + 2, :], in_=banks[2 * e + half][:])
-                        else:
-                            nc.scalar.copy(out=o_sb[:, 2 * half : 2 * half + 2, :], in_=banks[2 * e + half][:])
-                    d_cols = slice((2 * pair + e) * DPH, (2 * pair + e + 1) * DPH)
-                    nc.sync.dma_start(out=out[s].rearrange("(i p) d -> p i d", p=P)[:, :, d_cols], in_=o_sb[:])
+            def store(s, i, banks, scalar_helps):
+                o_sb = outputs.tile([P, H // 2, 2 * DPH], F32, tag="o_sb")
+                if not scalar_helps:
+                    nc.vector.tensor_copy(out=o_sb[:, 0, :], in_=banks[0][:].rearrange("p e d -> p (e d)"))
+                else:
+                    nc.scalar.copy(out=o_sb[:, 0, :], in_=banks[0][:].rearrange("p e d -> p (e d)"))
+                nc.vector.tensor_copy(out=o_sb[:, 1, :], in_=banks[1][:].rearrange("p e d -> p (e d)"))
+                nc.sync.dma_start(out=out[s, i * P : (i + 1) * P, :], in_=o_sb[:].rearrange("p a d -> p (a d)"))
 
-            for s in range(S):
-                for pair in range(H // 2):
-                    weights(s, pair)
+            tiles = [(s, i) for s in range(S) for i in reversed(range(NT))]
+            for s, i in tiles:
+                weights(s, i)
             for s in range(S):
                 project_values(s)
-            PAIRS = H // 2
-            pair_banks = []
-            for n in range(S * PAIRS + 1):
-                if n < S * PAIRS:
-                    pair_banks.append(multiply(n // PAIRS, n % PAIRS))
+            tile_banks = []
+            for n in range(len(tiles) + 1):
+                if n < len(tiles):
+                    tile_banks.append(multiply(tiles[n][0], tiles[n][1]))
                 if n > 0:
-                    store((n - 1) // PAIRS, (n - 1) % PAIRS, pair_banks[n - 1])
+                    store(tiles[n - 1][0], tiles[n - 1][1], tile_banks[n - 1], n - 1 >= VECTOR_TILES)

@@ -22,30 +22,22 @@ NT = B // P
 PASSES = D // (P * PACK)
 NW = D // P
 HEADS = S * H
-BANK_BLOCKS = 4
 VECTOR_TILES = 2
 PIECES = 3
-EXTRA = 2 * PIECES
 D2_FLOOR = 1e-12
 D2_CEIL = 2.0**64
+CANCELLED = 2.0**-22
+RUN = 4
 MASKED_LOG = 1e30
 
 FLOPS = 2 * S * B * D * D + 2 * S * H * B * B * DPP + 2 * S * H * B * B * DPH
-
-
-def first_column(i):
-    return P * (i * (i + 1) // 2)
-
-
-def query_tile(head, i):
-    return head[:, first_column(i) : first_column(i + 1)].rearrange("p (t b) -> p t b", t=i + 1)
 
 
 def tile_networklayer_pb_kernel(tc, q_pos, k_pos, x_grp, Wv, bv, out):
     nc = tc.nc
     with ExitStack() as ctx:
         keep = ctx.enter_context(tc.tile_pool(name="keep", bufs=1))
-        logs = ctx.enter_context(tc.tile_pool(name="logs", bufs=S))
+        banks = ctx.enter_context(tc.psum_pool(name="banks", bufs=8))
         ctx.enter_context(tc.manual_schedule())
 
         bias = keep.tile([P, D], BF16)
@@ -54,14 +46,11 @@ def tile_networklayer_pb_kernel(tc, q_pos, k_pos, x_grp, Wv, bv, out):
         v_codes = keep.tile([P, S, D], U32, align_bytes=64)
         v_scales = keep.tile([P, S, D], U8, align_bytes=64)
         w_bf = [keep.tile([P, NT, H, P, PACK], BF16, name="w_bf%d" % s, align_bytes=64) for s in range(S)]
-        group_logs = [logs.tile([P, H, first_column(NT)], F32, name="group_logs%d" % s, tag="group_logs") for s in range(S)]
+        logs = [keep.tile([P, NT, NT, H, P], F32, name="logs%d" % s) for s in range(S)]
 
         with ExitStack() as part_one:
             inputs = part_one.enter_context(tc.tile_pool(name="inputs", bufs=1))
-            small = part_one.enter_context(tc.tile_pool(name="small", bufs=2))
             stage = part_one.enter_context(tc.tile_pool(name="stage", bufs=3))
-            psum_t = part_one.enter_context(tc.psum_pool(name="psum_t", bufs=4))
-            psum_d = part_one.enter_context(tc.psum_pool(name="psum_d", bufs=4))
             q_nat = [inputs.tile([P, H, NT, DPP], BF16, name="q_nat%d" % s) for s in range(S)]
             k_nat = [inputs.tile([P, H, NT, DPP], BF16, name="k_nat%d" % s) for s in range(S)]
             w_nat = inputs.tile([P, NW, D], BF16)
@@ -71,12 +60,15 @@ def tile_networklayer_pb_kernel(tc, q_pos, k_pos, x_grp, Wv, bv, out):
                 nc.sync.dma_start(out=q_nat[s][:], in_=q_pos[s].rearrange("h (i p) f -> p h i f", p=P))
                 nc.sync.dma_start(out=k_nat[s][:], in_=k_pos[s].rearrange("h (i p) f -> p h i f", p=P))
 
-            load_positions(0)
+            for nat, dram in ((q_nat[0], q_pos[0]), (k_nat[0], k_pos[0])):
+                for h in range(H):
+                    nc.sync.dma_start(out=nat[:, h], in_=dram[h].rearrange("(i p) f -> p i f", p=P))
             w_rows = Wv.rearrange("(j p) k -> p j k", p=P)
             for half in range(2):
                 rows = slice(half * NW // 2, (half + 1) * NW // 2)
                 nc.sync.dma_start(out=w_nat[:, rows, :], in_=w_rows[:, rows, :])
-            load_positions(1)
+                if half == 0:
+                    load_positions(1)
             for s in range(S):
                 nc.sync.dma_start(out=x_nat[s][:], in_=x_grp[s].rearrange("(t p) k -> p t k", p=P))
             nc.sync.dma_start(out=bias[:], in_=bv.partition_broadcast(P))
@@ -89,76 +81,114 @@ def tile_networklayer_pb_kernel(tc, q_pos, k_pos, x_grp, Wv, bv, out):
             nc.vector.memset(one[:], 1.0)
             nc.scalar.activation(out=one[:], in_=one[:], func=ACT.Ln)
             q_feat = [inputs.tile([P, NT, P], BF16, name="q_feat%d" % s) for s in range(S)]
-            k_feat = [inputs.tile([P, NT, P], BF16, name="k_feat%d" % s) for s in range(S)]
-
-            def by_head(feat):
-                return feat[:, :, 0 : H * EXTRA].rearrange("p i (h j) -> p i h j", j=EXTRA)
-
             for s in range(S):
                 nc.vector.memset(q_feat[s][:], 0.0)
-                nc.vector.memset(by_head(q_feat[s])[:, :, :, PIECES:EXTRA], -0.5)
-                nc.vector.memset(k_feat[s][:], 0.0)
-                nc.vector.memset(by_head(k_feat[s])[:, :, :, 0:PIECES], -0.5)
-            for s in range(S):
-                for i in range(NT - 1):
-                    nc.gpsimd.memset(w_bf[s][:, i].rearrange("p h b t -> p (h b t)").bitcast(F32), 0.0)
             head_rows = inputs.tile([P, H], F32)
             nc.vector.tensor_reduce(
                 out=head_rows[:],
-                in_=ident_f32[:, 0 : H * EXTRA].rearrange("p (h j) -> p h j", j=EXTRA),
+                in_=ident_f32[:, 0 : H * PIECES].rearrange("p (h j) -> p h j", j=PIECES),
                 axis=AX.X,
                 op=ALU.add,
             )
+            minus_half = inputs.tile([P, H, P], BF16)
+            nc.vector.tensor_scalar(
+                out=minus_half[:],
+                in0=head_rows[:].unsqueeze(2).to_broadcast([P, H, P]),
+                scalar1=-0.5,
+                scalar2=None,
+                op0=ALU.mult,
+            )
+            for s in range(S):
+                for i in range(NT - 1):
+                    nc.gpsimd.memset(w_bf[s][:, i].rearrange("p h b t -> p (h b t)").bitcast(F32), 0.0)
 
             qkT = inputs.tile([P, S, H, 2, B], BF16)
             q_extra = inputs.tile([P, S, B], BF16)
-            k_extra = inputs.tile([P, S, H, B], BF16)
+            k_squares = inputs.tile([P, S, H * NT], F32)
+            upper = inputs.tile([P, S, H * NT], F32)
+            lower = inputs.tile([P, S, H * NT], F32)
 
-            def sums_of_squares(nat, name):
-                squares = small.tile([P, H * NT, DPP], F32, tag="squares")
-                nc.scalar.activation(out=squares[:], in_=nat[:].rearrange("p h i f -> p (h i) f"), func=ACT.Square)
-                sums = inputs.tile([P, H * NT], F32, name=name)
-                nc.vector.tensor_reduce(out=sums[:], in_=squares[:], axis=AX.X, op=ALU.add)
-                return sums
+            def statistics(nat, name):
+                stats = inputs.tile([P, H * NT, 3], F32, name=name)
+                by_call = stats[:].rearrange("p (c e) k -> p c (e k)", e=2)
+                pairs = nat[:].rearrange("p h (c e) f -> p (h c) f e", e=2)
+                calls = [
+                    lambda c=c: nc.vector.bn_stats(out=by_call[:, c, :], in_=pairs[:, c]) for c in range(H * NT // 2)
+                ]
+                return stats, calls
 
-            def extra_features(s):
-                q_sums = sums_of_squares(q_nat[s], "q_sums%d" % s)
-                k_sums = sums_of_squares(k_nat[s], "k_sums%d" % s)
-                split_in_pieces(q_sums, q_feat[s], 0)
-                split_in_pieces(k_sums, k_feat[s], PIECES)
+            def square_of_mean(stats, name):
+                part = inputs.tile([P, H * NT], F32, name=name)
+                step = lambda: nc.vector.scalar_tensor_tensor(
+                    out=part[:], in0=stats[:, :, 1], scalar=float(DPP), in1=stats[:, :, 1], op0=ALU.mult, op1=ALU.mult
+                )
+                return part, step
+
+            def query_steps(s, stats, piece_engine):
+                part, first_step = square_of_mean(stats, "q_part%d" % s)
+                sums = inputs.tile([P, H * NT], F32, name="q_sums%d" % s)
+                steps = [
+                    first_step,
+                    lambda: nc.vector.tensor_tensor(out=sums[:], in0=stats[:, :, 2], in1=part[:], op=ALU.add),
+                ]
+                rest = sums[:].rearrange("p (h i) -> p i h", i=NT)
+                for j in range(PIECES):
+                    piece = q_feat[s][:, :, 0 : H * PIECES].rearrange("p i (h j) -> p i h j", j=PIECES)[:, :, :, j]
+                    steps.append(lambda piece=piece, rest=rest: piece_engine.tensor_copy(out=piece, in_=rest))
+                    if j < PIECES - 1:
+                        left = inputs.tile([P, NT, H], F32, name="left%d_%d" % (s, j))
+                        steps.append(
+                            lambda left=left, piece=piece, rest=rest: piece_engine.tensor_tensor(
+                                out=left[:], in0=rest, in1=piece, op=ALU.subtract
+                            )
+                        )
+                        rest = left[:]
+                return steps
+
+            def key_steps(s, stats):
+                part, first_step = square_of_mean(stats, "k_part%d" % s)
+                return [
+                    first_step,
+                    lambda: nc.vector.scalar_tensor_tensor(
+                        out=k_squares[:, s, :], in0=stats[:, :, 2], scalar=D2_FLOOR, in1=part[:], op0=ALU.add, op1=ALU.add
+                    ),
+                    lambda: nc.vector.tensor_scalar(
+                        out=upper[:, s, :], in0=k_squares[:, s, :], scalar1=0.5 * (1.0 - CANCELLED), scalar2=None, op0=ALU.mult
+                    ),
+                    lambda: nc.vector.tensor_scalar(
+                        out=lower[:, s, :],
+                        in0=k_squares[:, s, :],
+                        scalar1=0.5,
+                        scalar2=0.5 * D2_CEIL,
+                        op0=ALU.mult,
+                        op1=ALU.subtract,
+                    ),
+                ]
+
+            def run_in_turns(calls, steps):
+                for n in range(max(len(calls), len(steps))):
+                    if n < len(calls):
+                        calls[n]()
+                    if n < len(steps):
+                        steps[n]()
 
             def transposed(blocks):
-                tp = psum_t.tile([P, NT, P], BF16, tag="tp")
+                tp = banks.tile([P, NT, P], BF16, tag="bank")
                 for i in range(NT):
                     nc.tensor.transpose(tp[:, i, :], blocks[:, i, :], ident_bf[:])
                 return tp[:].rearrange("p i b -> p (i b)")
 
             def transpose_positions(s):
                 for h in range(H):
-                    tp = psum_t.tile([P, 2, NT, P], BF16, tag="tp")
+                    tp = banks.tile([P, 2, NT, P], BF16, tag="bank")
                     for i in range(NT):
                         nc.tensor.transpose(tp[:, 0, i, :], q_nat[s][:, h, i, :], ident_bf[:])
                     for i in range(NT):
                         nc.tensor.transpose(tp[:, 1, i, :], k_nat[s][:, h, i, :], ident_bf[:])
                     nc.scalar.copy(out=qkT[:, s, h], in_=tp[:].rearrange("p x i b -> p x (i b)"))
 
-            def split_in_pieces(sums, feat, first):
-                rest = sums[:].rearrange("p (h i) -> p i h", i=NT)
-                for j in range(PIECES):
-                    piece = by_head(feat)[:, :, :, first + j]
-                    nc.vector.tensor_copy(out=piece, in_=rest)
-                    if j < PIECES - 1:
-                        left = small.tile([P, NT, H], F32, tag="left")
-                        nc.vector.tensor_tensor(out=left[:], in0=rest, in1=piece, op=ALU.subtract)
-                        rest = left[:]
-
             def transpose_extra_features(s):
                 nc.vector.tensor_copy(out=q_extra[:, s, :], in_=transposed(q_feat[s]))
-                k_rows = transposed(k_feat[s])
-                for h in range(H):
-                    nc.vector.tensor_scalar(
-                        out=k_extra[:, s, h, :], in0=k_rows, scalar1=head_rows[:, h : h + 1], scalar2=None, op0=ALU.mult
-                    )
 
             def row_tile(n):
                 if n < NW:
@@ -170,7 +200,7 @@ def tile_networklayer_pb_kernel(tc, q_pos, k_pos, x_grp, Wv, bv, out):
                 words = grouped[:].bitcast(F32).rearrange("p (n g r u) -> p n g r u", n=2, g=PASSES, u=2)
                 for n in range(2):
                     source = row_tile(2 * pair + n).bitcast(F32)
-                    tp = psum_t.tile([P, PASSES, 2, P], F32, tag="tp")
+                    tp = banks.tile([P, PASSES, 2, P], F32, tag="bank")
                     for g in range(PASSES):
                         for u in range(2):
                             first = (2 * g + u) * P
@@ -186,68 +216,73 @@ def tile_networklayer_pb_kernel(tc, q_pos, k_pos, x_grp, Wv, bv, out):
                     in_=grouped[:],
                 )
 
-            def distances(s, h):
-                logd = group_logs[s][:, h, :]
-                blocks = [(i, t) for i in range(NT) for t in range(i + 1)]
-                for first in range(0, len(blocks), BANK_BLOCKS):
-                    in_bank = blocks[first : first + BANK_BLOCKS]
-                    dots = psum_d.tile([P, BANK_BLOCKS, P], F32, tag="dots")
-                    for m, (i, t) in enumerate(in_bank):
-                        b_cols = slice(i * P, (i + 1) * P)
-                        c_cols = slice(t * P, (t + 1) * P)
-                        nc.tensor.matmul(
-                            out=dots[:, m, :],
-                            lhsT=qkT[:, s, h, 1, c_cols],
-                            rhs=qkT[:, s, h, 0, b_cols],
-                            start=True,
-                            stop=False,
-                        )
-                        nc.tensor.matmul(
-                            out=dots[:, m, :],
-                            lhsT=k_extra[:, s, h, c_cols],
-                            rhs=q_extra[:, s, b_cols],
-                            start=False,
-                            stop=True,
-                        )
-                    nc.vector.tensor_scalar(
-                        out=logd[:, first * P : (first + len(in_bank)) * P],
-                        in0=dots[:, 0 : len(in_bank), :].rearrange("p m b -> p (m b)"),
-                        scalar1=-0.5 * D2_FLOOR,
-                        scalar2=-0.5 * D2_CEIL,
-                        op0=ALU.min,
-                        op1=ALU.max,
-                    )
-                return logd
+            def distances(s, h, t):
+                live = slice(t * P, B)
+                column = slice(h * NT + t, h * NT + t + 1)
+                dots = banks.tile([P, B], F32, tag="bank")
+                nc.tensor.matmul(
+                    out=dots[:, live], lhsT=qkT[:, s, h, 1, t * P : (t + 1) * P], rhs=qkT[:, s, h, 0, live], start=True, stop=False
+                )
+                nc.tensor.matmul(
+                    out=dots[:, live], lhsT=minus_half[:, h, :], rhs=q_extra[:, s, live], start=False, stop=True
+                )
+                nc.vector.tensor_scalar(
+                    out=logs[s][:, t, t:NT, h, :],
+                    in0=dots[:, live].rearrange("p (i b) -> p i b", b=P),
+                    scalar1=upper[:, s, column],
+                    scalar2=lower[:, s, column],
+                    op0=ALU.min,
+                    op1=ALU.max,
+                )
 
-            def logarithms(logd):
-                nc.scalar.activation(out=logd, in_=logd, func=ACT.Ln, scale=-2.0)
-                for i in range(NT):
-                    diagonal = query_tile(logd, i)[:, i, :]
-                    nc.gpsimd.affine_select(
-                        out=diagonal,
-                        in_=diagonal,
-                        pattern=[[1, P]],
-                        compare_op=ALU.is_ge,
-                        fill=MASKED_LOG,
-                        base=0,
-                        channel_multiplier=-1,
-                    )
+            def logarithm(s, h, t):
+                logd = logs[s][:, t, t:NT, h, :]
+                nc.scalar.activation(
+                    out=logd,
+                    in_=logd,
+                    func=ACT.Ln,
+                    scale=-2.0,
+                    bias=k_squares[:, s, h * NT + t : h * NT + t + 1],
+                )
 
-            extra_features(0)
+            def mask(s, t):
+                diagonal = logs[s][:, t, t]
+                nc.gpsimd.affine_select(
+                    out=diagonal,
+                    in_=diagonal,
+                    pattern=[[0, H], [1, P]],
+                    compare_op=ALU.is_ge,
+                    fill=MASKED_LOG,
+                    base=0,
+                    channel_multiplier=-1,
+                )
+
+            q_stats, q_calls = statistics(q_nat[0], "q_stats0")
+            k_stats, k_calls = statistics(k_nat[0], "k_stats0")
+            for call in q_calls:
+                call()
+            run_in_turns(k_calls, query_steps(0, q_stats, nc.vector))
+            for step in key_steps(0, k_stats):
+                step()
             transpose_positions(0)
             transpose_extra_features(0)
 
+            q_stats, q_calls = statistics(q_nat[1], "q_stats1")
+            k_stats, k_calls = statistics(k_nat[1], "k_stats1")
+            beside = {1: q_calls, 2: query_steps(1, q_stats, nc.gpsimd) + k_calls, 3: key_steps(1, k_stats)}
             row_pairs = []
             for n in range(HEADS):
+                s, h = n // H, n % H
+                run_in_turns([lambda t=t: distances(s, h, t) for t in range(NT)], beside.get(n, []))
                 row_pairs.append(transpose_rows(n))
-                logd = distances(n // H, n % H)
-                if n == 0:
-                    extra_features(1)
-                if n == 1:
-                    transpose_positions(1)
                 if n == 2:
+                    transpose_positions(1)
+                if n == 3:
                     transpose_extra_features(1)
-                logarithms(logd)
+                for t in range(NT):
+                    logarithm(s, h, t)
+                    if h == H - 1:
+                        mask(s, t)
                 if n > 0:
                     quantise_rows(n - 1, row_pairs[n - 1])
             quantise_rows(HEADS - 1, row_pairs[HEADS - 1])
@@ -255,14 +290,11 @@ def tile_networklayer_pb_kernel(tc, q_pos, k_pos, x_grp, Wv, bv, out):
         with ExitStack() as part_two:
             outputs = part_two.enter_context(tc.tile_pool(name="outputs", bufs=HEADS))
             work = part_two.enter_context(tc.tile_pool(name="work", bufs=2))
-            psum_v = part_two.enter_context(tc.psum_pool(name="psum_v", bufs=4))
-            psum_o = part_two.enter_context(tc.psum_pool(name="psum_o", bufs=4))
 
             def weights(s, i):
-                logd = group_logs[s][:, :, first_column(i) : first_column(i + 1)]
                 nc.scalar.activation(
-                    out=w_bf[s][:, i, :, :, 0 : i + 1],
-                    in_=logd.rearrange("p h (t b) -> p h b t", t=i + 1),
+                    out=w_bf[s][:, i].rearrange("p h b t -> p (h b) t")[:, :, 0 : i + 1].rearrange("p (c j) t -> p c t j", j=RUN),
+                    in_=logs[s][:, 0 : i + 1, i].rearrange("p t h b -> p t (h b)").rearrange("p t (c j) -> p c t j", j=RUN),
                     func=ACT.Sigmoid,
                     scale=-0.5,
                 )
@@ -270,7 +302,7 @@ def tile_networklayer_pb_kernel(tc, q_pos, k_pos, x_grp, Wv, bv, out):
             def project_values(s):
                 v_bf = work.tile([P, NW, P, PACK], BF16, tag="v_bf", align_bytes=64)
                 for j in range(NW):
-                    v_ps = psum_v.tile([P, NT, P], F32, tag="v_ps")
+                    v_ps = banks.tile([P, NT, P], F32, tag="bank")
                     for t in range(NT):
                         for g in range(PASSES):
                             nc.tensor.matmul_mx(
@@ -302,9 +334,9 @@ def tile_networklayer_pb_kernel(tc, q_pos, k_pos, x_grp, Wv, bv, out):
                     scales=w_scales[:].rearrange("p h b -> p (h b)"),
                     in_=w_bf[s][:, i].rearrange("p h b t -> p (h b t)"),
                 )
-                banks = []
+                products = []
                 for pair in range(H // 2):
-                    o_ps = psum_o.tile([P, 2, DPH], F32, tag="o_ps")
+                    o_ps = banks.tile([P, 2, DPH], F32, tag="bank")
                     for e in range(2):
                         h = 2 * pair + e
                         d_cols = slice(h * DPH, (h + 1) * DPH)
@@ -317,16 +349,16 @@ def tile_networklayer_pb_kernel(tc, q_pos, k_pos, x_grp, Wv, bv, out):
                             start=True,
                             stop=True,
                         )
-                    banks.append(o_ps)
-                return banks
+                    products.append(o_ps)
+                return products
 
-            def store(s, i, banks, scalar_helps):
+            def store(s, i, products, scalar_helps):
                 o_sb = outputs.tile([P, H // 2, 2 * DPH], F32, tag="o_sb")
                 if not scalar_helps:
-                    nc.vector.tensor_copy(out=o_sb[:, 0, :], in_=banks[0][:].rearrange("p e d -> p (e d)"))
+                    nc.vector.tensor_copy(out=o_sb[:, 0, :], in_=products[0][:].rearrange("p e d -> p (e d)"))
                 else:
-                    nc.scalar.copy(out=o_sb[:, 0, :], in_=banks[0][:].rearrange("p e d -> p (e d)"))
-                nc.vector.tensor_copy(out=o_sb[:, 1, :], in_=banks[1][:].rearrange("p e d -> p (e d)"))
+                    nc.scalar.copy(out=o_sb[:, 0, :], in_=products[0][:].rearrange("p e d -> p (e d)"))
+                nc.vector.tensor_copy(out=o_sb[:, 1, :], in_=products[1][:].rearrange("p e d -> p (e d)"))
                 nc.sync.dma_start(out=out[s, i * P : (i + 1) * P, :], in_=o_sb[:].rearrange("p a d -> p (a d)"))
 
             tiles = [(s, i) for s in range(S) for i in reversed(range(NT))]
@@ -334,9 +366,9 @@ def tile_networklayer_pb_kernel(tc, q_pos, k_pos, x_grp, Wv, bv, out):
                 weights(s, i)
             for s in range(S):
                 project_values(s)
-            tile_banks = []
+            tile_products = []
             for n in range(len(tiles) + 1):
                 if n < len(tiles):
-                    tile_banks.append(multiply(tiles[n][0], tiles[n][1]))
+                    tile_products.append(multiply(tiles[n][0], tiles[n][1]))
                 if n > 0:
-                    store(tiles[n - 1][0], tiles[n - 1][1], tile_banks[n - 1], n - 1 >= VECTOR_TILES)
+                    store(tiles[n - 1][0], tiles[n - 1][1], tile_products[n - 1], n - 1 >= VECTOR_TILES)

@@ -22,7 +22,11 @@ NT = B // P
 PASSES = D // (P * PACK)
 NW = D // P
 HEADS = S * H
-VECTOR_TILES = 2
+VECTOR_BANKS = (2, 2, 1, 1, 1, 1, 1, 1)
+QJ = 4
+NB = 1
+NP = 2
+NX = 3
 PIECES = 3
 D2_FLOOR = 1e-12
 D2_CEIL = 2.0**64
@@ -47,6 +51,71 @@ def tile_networklayer_pb_kernel(tc, q_pos, k_pos, x_grp, Wv, bv, out):
         v_scales = keep.tile([P, S, D], U8, align_bytes=64)
         w_bf = [keep.tile([P, NT, H, P, PACK], BF16, name="w_bf%d" % s, align_bytes=64) for s in range(S)]
         logs = [keep.tile([P, NT, NT, H, P], F32, name="logs%d" % s) for s in range(S)]
+
+        work = ctx.enter_context(tc.tile_pool(name="work", bufs=2))
+
+        def weights(s, i):
+            nc.scalar.activation(
+                out=w_bf[s][:, i].rearrange("p h b t -> p (h b) t")[:, :, 0 : i + 1].rearrange("p (c j) t -> p c t j", j=RUN),
+                in_=logs[s][:, 0 : i + 1, i].rearrange("p t h b -> p t (h b)").rearrange("p t (c j) -> p c t j", j=RUN),
+                func=ACT.Sigmoid,
+                scale=-0.5,
+            )
+
+        def project_values(s, beside):
+            v_bf = work.tile([P, NW, P, PACK], BF16, tag="v_bf", align_bytes=64)
+            for j in range(NW):
+                v_ps = banks.tile([P, NT, P], F32, tag="bank")
+                for t in range(NT):
+                    for g in range(PASSES):
+                        nc.tensor.matmul_mx(
+                            out=v_ps[:, t, :],
+                            lhsT=xw_codes[:, NW + NT * s + t, g, :].bitcast(FP8X4),
+                            lhsT_scale=xw_scales[:, NW + NT * s + t, g, :],
+                            rhs=xw_codes[:, j, g, :].bitcast(FP8X4),
+                            rhs_scale=xw_scales[:, j, g, :],
+                            start=(g == 0),
+                            stop=(g == PASSES - 1),
+                        )
+                for step in beside.get(j, []):
+                    step()
+                nc.vector.tensor_tensor(
+                    out=v_bf[:, j],
+                    in0=v_ps[:].rearrange("p t d -> p d t"),
+                    in1=bias[:, j * P : (j + 1) * P].unsqueeze(2).to_broadcast([P, P, PACK]),
+                    op=ALU.add,
+                )
+            nc.vector.quantize_mx(
+                out=v_codes[:, s, :].bitcast(FP8X4),
+                scales=v_scales[:, s, :],
+                in_=v_bf[:].rearrange("p j d t -> p (j d t)"),
+            )
+
+        def multiply(s, i):
+            w_codes = work.tile([P, H, P], U32, tag="w_codes", align_bytes=64)
+            w_scales = work.tile([P, H, P], U8, tag="w_scales", align_bytes=64)
+            nc.vector.quantize_mx(
+                out=w_codes[:].rearrange("p h b -> p (h b)").bitcast(FP8X4),
+                scales=w_scales[:].rearrange("p h b -> p (h b)"),
+                in_=w_bf[s][:, i].rearrange("p h b t -> p (h b t)"),
+            )
+            products = []
+            for pair in range(H // 2):
+                o_ps = banks.tile([P, 2, DPH], F32, tag="bank")
+                for e in range(2):
+                    h = 2 * pair + e
+                    d_cols = slice(h * DPH, (h + 1) * DPH)
+                    nc.tensor.matmul_mx(
+                        out=o_ps[:, e, :],
+                        lhsT=w_codes[:, h, :].bitcast(FP8X4),
+                        lhsT_scale=w_scales[:, h, :],
+                        rhs=v_codes[:, s, d_cols].bitcast(FP8X4),
+                        rhs_scale=v_scales[:, s, d_cols],
+                        start=True,
+                        stop=True,
+                    )
+                products.append(o_ps)
+            return products
 
         with ExitStack() as part_one:
             inputs = part_one.enter_context(tc.tile_pool(name="inputs", bufs=1))
@@ -98,9 +167,6 @@ def tile_networklayer_pb_kernel(tc, q_pos, k_pos, x_grp, Wv, bv, out):
                 scalar2=None,
                 op0=ALU.mult,
             )
-            for s in range(S):
-                for i in range(NT - 1):
-                    nc.gpsimd.memset(w_bf[s][:, i].rearrange("p h b t -> p (h b t)").bitcast(F32), 0.0)
 
             qkT = inputs.tile([P, S, H, 2, B], BF16)
             q_extra = inputs.tile([P, S, B], BF16)
@@ -109,59 +175,53 @@ def tile_networklayer_pb_kernel(tc, q_pos, k_pos, x_grp, Wv, bv, out):
             lower = inputs.tile([P, S, H * NT], F32)
 
             def statistics(nat, name):
-                stats = inputs.tile([P, H * NT, 3], F32, name=name)
+                stats = inputs.tile([P, H * NT, 3], F32, name=name + "_stats")
+                part = inputs.tile([P, H * NT], F32, name=name + "_part")
+                sums = inputs.tile([P, H * NT], F32, name=name + "_sums")
                 by_call = stats[:].rearrange("p (c e) k -> p c (e k)", e=2)
                 pairs = nat[:].rearrange("p h (c e) f -> p (h c) f e", e=2)
                 calls = [
                     lambda c=c: nc.vector.bn_stats(out=by_call[:, c, :], in_=pairs[:, c]) for c in range(H * NT // 2)
                 ]
-                return stats, calls
-
-            def square_of_mean(stats, name):
-                part = inputs.tile([P, H * NT], F32, name=name)
-                step = lambda: nc.vector.scalar_tensor_tensor(
-                    out=part[:], in0=stats[:, :, 1], scalar=float(DPP), in1=stats[:, :, 1], op0=ALU.mult, op1=ALU.mult
-                )
-                return part, step
-
-            def query_steps(s, stats, piece_engine):
-                part, first_step = square_of_mean(stats, "q_part%d" % s)
-                sums = inputs.tile([P, H * NT], F32, name="q_sums%d" % s)
                 steps = [
-                    first_step,
+                    lambda: nc.vector.scalar_tensor_tensor(
+                        out=part[:], in0=stats[:, :, 1], scalar=float(DPP), in1=stats[:, :, 1], op0=ALU.mult, op1=ALU.mult
+                    ),
                     lambda: nc.vector.tensor_tensor(out=sums[:], in0=stats[:, :, 2], in1=part[:], op=ALU.add),
                 ]
-                rest = sums[:].rearrange("p (h i) -> p i h", i=NT)
-                for j in range(PIECES):
-                    piece = q_feat[s][:, :, 0 : H * PIECES].rearrange("p i (h j) -> p i h j", j=PIECES)[:, :, :, j]
-                    steps.append(lambda piece=piece, rest=rest: piece_engine.tensor_copy(out=piece, in_=rest))
-                    if j < PIECES - 1:
-                        left = inputs.tile([P, NT, H], F32, name="left%d_%d" % (s, j))
-                        steps.append(
-                            lambda left=left, piece=piece, rest=rest: piece_engine.tensor_tensor(
-                                out=left[:], in0=rest, in1=piece, op=ALU.subtract
-                            )
-                        )
-                        rest = left[:]
-                return steps
+                return sums, calls, steps
 
-            def key_steps(s, stats):
-                part, first_step = square_of_mean(stats, "k_part%d" % s)
+            def query_pieces(s, sums, engine):
+                pieces = q_feat[s][:, :, 0 : H * PIECES].rearrange("p i (h j) -> p i h j", j=PIECES)
+                whole = sums[:].rearrange("p (h i) -> p i h", i=NT)
+                left = inputs.tile([P, NT, H], F32, name="left%d" % s)
                 return [
-                    first_step,
-                    lambda: nc.vector.scalar_tensor_tensor(
-                        out=k_squares[:, s, :], in0=stats[:, :, 2], scalar=D2_FLOOR, in1=part[:], op0=ALU.add, op1=ALU.add
+                    lambda: engine.tensor_copy(out=pieces[:, :, :, 0], in_=whole),
+                    lambda: engine.tensor_tensor(out=left[:], in0=whole, in1=pieces[:, :, :, 0], op=ALU.subtract),
+                    lambda: engine.tensor_tensor(out=pieces[:, :, :, 1], in0=whole, in1=pieces[:, :, :, 0], op=ALU.subtract),
+                    lambda: engine.tensor_tensor(out=pieces[:, :, :, 2], in0=left[:], in1=pieces[:, :, :, 1], op=ALU.subtract),
+                ]
+
+            def key_columns(s, sums):
+                return [
+                    lambda: nc.gpsimd.tensor_scalar(
+                        out=upper[:, s, :],
+                        in0=sums[:],
+                        scalar1=D2_FLOOR,
+                        scalar2=0.5 * (1.0 - CANCELLED),
+                        op0=ALU.add,
+                        op1=ALU.mult,
                     ),
-                    lambda: nc.vector.tensor_scalar(
-                        out=upper[:, s, :], in0=k_squares[:, s, :], scalar1=0.5 * (1.0 - CANCELLED), scalar2=None, op0=ALU.mult
-                    ),
-                    lambda: nc.vector.tensor_scalar(
+                    lambda: nc.gpsimd.tensor_scalar(
                         out=lower[:, s, :],
-                        in0=k_squares[:, s, :],
+                        in0=sums[:],
                         scalar1=0.5,
                         scalar2=0.5 * D2_CEIL,
                         op0=ALU.mult,
                         op1=ALU.subtract,
+                    ),
+                    lambda: nc.gpsimd.tensor_scalar(
+                        out=k_squares[:, s, :], in0=sums[:], scalar1=D2_FLOOR, scalar2=None, op0=ALU.add
                     ),
                 ]
 
@@ -188,7 +248,7 @@ def tile_networklayer_pb_kernel(tc, q_pos, k_pos, x_grp, Wv, bv, out):
                     nc.scalar.copy(out=qkT[:, s, h], in_=tp[:].rearrange("p x i b -> p x (i b)"))
 
             def transpose_extra_features(s):
-                nc.vector.tensor_copy(out=q_extra[:, s, :], in_=transposed(q_feat[s]))
+                nc.scalar.copy(out=q_extra[:, s, :], in_=transposed(q_feat[s]))
 
             def row_tile(n):
                 if n < NW:
@@ -257,27 +317,35 @@ def tile_networklayer_pb_kernel(tc, q_pos, k_pos, x_grp, Wv, bv, out):
                     channel_multiplier=-1,
                 )
 
-            q_stats, q_calls = statistics(q_nat[0], "q_stats0")
-            k_stats, k_calls = statistics(k_nat[0], "k_stats0")
+            q_sums, q_calls, q_steps = statistics(q_nat[0], "q0")
+            transpose_positions(0)
+            k_sums, k_calls, k_steps = statistics(k_nat[0], "k0")
             for call in q_calls:
                 call()
-            run_in_turns(k_calls, query_steps(0, q_stats, nc.vector))
-            for step in key_steps(0, k_stats):
+            run_in_turns(k_calls, q_steps + query_pieces(0, q_sums, nc.vector))
+            for step in k_steps + key_columns(0, k_sums):
                 step()
-            transpose_positions(0)
             transpose_extra_features(0)
 
-            q_stats, q_calls = statistics(q_nat[1], "q_stats1")
-            k_stats, k_calls = statistics(k_nat[1], "k_stats1")
-            beside = {1: q_calls, 2: query_steps(1, q_stats, nc.gpsimd) + k_calls, 3: key_steps(1, k_stats)}
+            for s in range(S):
+                for i in range(NT - 1):
+                    nc.gpsimd.memset(w_bf[s][:, i].rearrange("p h b t -> p (h b t)").bitcast(F32), 0.0)
+
+            q_sums, q_calls, q_steps = statistics(q_nat[1], "q1")
+            k_sums, k_calls, k_steps = statistics(k_nat[1], "k1")
+            beside = {
+                NB: q_calls,
+                NB + 1: q_steps + k_calls,
+                NB + 2: query_pieces(1, q_sums, nc.gpsimd) + k_steps + key_columns(1, k_sums),
+            }
             row_pairs = []
             for n in range(HEADS):
                 s, h = n // H, n % H
                 run_in_turns([lambda t=t: distances(s, h, t) for t in range(NT)], beside.get(n, []))
                 row_pairs.append(transpose_rows(n))
-                if n == 2:
+                if n == NP:
                     transpose_positions(1)
-                if n == 3:
+                if n == NX:
                     transpose_extra_features(1)
                 for t in range(NT):
                     logarithm(s, h, t)
@@ -285,90 +353,30 @@ def tile_networklayer_pb_kernel(tc, q_pos, k_pos, x_grp, Wv, bv, out):
                         mask(s, t)
                 if n > 0:
                     quantise_rows(n - 1, row_pairs[n - 1])
-            quantise_rows(HEADS - 1, row_pairs[HEADS - 1])
+            for i in reversed(range(NT)):
+                weights(0, i)
+            project_values(0, {QJ: [lambda: quantise_rows(HEADS - 1, row_pairs[HEADS - 1])]})
 
-        with ExitStack() as part_two:
-            outputs = part_two.enter_context(tc.tile_pool(name="outputs", bufs=HEADS))
-            work = part_two.enter_context(tc.tile_pool(name="work", bufs=2))
+        outputs = ctx.enter_context(tc.tile_pool(name="outputs", bufs=HEADS))
 
-            def weights(s, i):
-                nc.scalar.activation(
-                    out=w_bf[s][:, i].rearrange("p h b t -> p (h b) t")[:, :, 0 : i + 1].rearrange("p (c j) t -> p c t j", j=RUN),
-                    in_=logs[s][:, 0 : i + 1, i].rearrange("p t h b -> p t (h b)").rearrange("p t (c j) -> p c t j", j=RUN),
-                    func=ACT.Sigmoid,
-                    scale=-0.5,
-                )
-
-            def project_values(s):
-                v_bf = work.tile([P, NW, P, PACK], BF16, tag="v_bf", align_bytes=64)
-                for j in range(NW):
-                    v_ps = banks.tile([P, NT, P], F32, tag="bank")
-                    for t in range(NT):
-                        for g in range(PASSES):
-                            nc.tensor.matmul_mx(
-                                out=v_ps[:, t, :],
-                                lhsT=xw_codes[:, NW + NT * s + t, g, :].bitcast(FP8X4),
-                                lhsT_scale=xw_scales[:, NW + NT * s + t, g, :],
-                                rhs=xw_codes[:, j, g, :].bitcast(FP8X4),
-                                rhs_scale=xw_scales[:, j, g, :],
-                                start=(g == 0),
-                                stop=(g == PASSES - 1),
-                            )
-                    nc.vector.tensor_tensor(
-                        out=v_bf[:, j],
-                        in0=v_ps[:].rearrange("p t d -> p d t"),
-                        in1=bias[:, j * P : (j + 1) * P].unsqueeze(2).to_broadcast([P, P, PACK]),
-                        op=ALU.add,
-                    )
-                nc.vector.quantize_mx(
-                    out=v_codes[:, s, :].bitcast(FP8X4),
-                    scales=v_scales[:, s, :],
-                    in_=v_bf[:].rearrange("p j d t -> p (j d t)"),
-                )
-
-            def multiply(s, i):
-                w_codes = work.tile([P, H, P], U32, tag="w_codes", align_bytes=64)
-                w_scales = work.tile([P, H, P], U8, tag="w_scales", align_bytes=64)
-                nc.vector.quantize_mx(
-                    out=w_codes[:].rearrange("p h b -> p (h b)").bitcast(FP8X4),
-                    scales=w_scales[:].rearrange("p h b -> p (h b)"),
-                    in_=w_bf[s][:, i].rearrange("p h b t -> p (h b t)"),
-                )
-                products = []
-                for pair in range(H // 2):
-                    o_ps = banks.tile([P, 2, DPH], F32, tag="bank")
-                    for e in range(2):
-                        h = 2 * pair + e
-                        d_cols = slice(h * DPH, (h + 1) * DPH)
-                        nc.tensor.matmul_mx(
-                            out=o_ps[:, e, :],
-                            lhsT=w_codes[:, h, :].bitcast(FP8X4),
-                            lhsT_scale=w_scales[:, h, :],
-                            rhs=v_codes[:, s, d_cols].bitcast(FP8X4),
-                            rhs_scale=v_scales[:, s, d_cols],
-                            start=True,
-                            stop=True,
-                        )
-                    products.append(o_ps)
-                return products
-
-            def store(s, i, products, scalar_helps):
-                o_sb = outputs.tile([P, H // 2, 2 * DPH], F32, tag="o_sb")
-                if not scalar_helps:
-                    nc.vector.tensor_copy(out=o_sb[:, 0, :], in_=products[0][:].rearrange("p e d -> p (e d)"))
+        def store(s, i, products, n):
+            o_sb = outputs.tile([P, H // 2, 2 * DPH], F32, tag="o_sb")
+            for half in range(2):
+                source = products[half][:].rearrange("p e d -> p (e d)")
+                if half >= VECTOR_BANKS[n]:
+                    nc.scalar.copy(out=o_sb[:, half, :], in_=source)
                 else:
-                    nc.scalar.copy(out=o_sb[:, 0, :], in_=products[0][:].rearrange("p e d -> p (e d)"))
-                nc.vector.tensor_copy(out=o_sb[:, 1, :], in_=products[1][:].rearrange("p e d -> p (e d)"))
-                nc.sync.dma_start(out=out[s, i * P : (i + 1) * P, :], in_=o_sb[:].rearrange("p a d -> p (a d)"))
+                    nc.vector.tensor_copy(out=o_sb[:, half, :], in_=source)
+                d_cols = slice(half * 2 * DPH, (half + 1) * 2 * DPH)
+                nc.sync.dma_start(out=out[s, i * P : (i + 1) * P, d_cols], in_=o_sb[:, half, :])
 
-            tiles = [(s, i) for s in range(S) for i in reversed(range(NT))]
-            for s, i in tiles:
-                weights(s, i)
-            for s in range(S):
-                project_values(s)
-            tile_products = []
-            for n in range(len(tiles) + 1):
-                if n < len(tiles):
-                    tile_products.append(multiply(tiles[n][0], tiles[n][1]))
-                if n > 0:
-                    store(tiles[n - 1][0], tiles[n - 1][1], tile_products[n - 1], n - 1 >= VECTOR_TILES)
+        for i in reversed(range(NT)):
+            weights(1, i)
+        project_values(1, {})
+        tiles = [(s, i) for s in range(S) for i in reversed(range(NT))]
+        tile_products = []
+        for n in range(len(tiles) + 1):
+            if n < len(tiles):
+                tile_products.append(multiply(tiles[n][0], tiles[n][1]))
+            if n > 0:
+                store(tiles[n - 1][0], tiles[n - 1][1], tile_products[n - 1], n - 1)

@@ -126,12 +126,13 @@ def tile_networklayer_pb_kernel(tc, q_pos, k_pos, x_grp, Wv, bv, out):
             x_nat = [inputs.tile([P, NT, D], BF16, name="x_nat%d" % s) for s in range(S)]
 
             def load_positions(s):
-                nc.sync.dma_start(out=q_nat[s][:], in_=q_pos[s].rearrange("h (i p) f -> p h i f", p=P))
+                nc.sync.dma_start(out=q_nat[s][:], in_=q_pos[s].rearrange("h (p i) f -> p h i f", p=P))
                 nc.sync.dma_start(out=k_nat[s][:], in_=k_pos[s].rearrange("h (i p) f -> p h i f", p=P))
 
-            for nat, dram in ((q_nat[0], q_pos[0]), (k_nat[0], k_pos[0])):
-                for h in range(H):
-                    nc.sync.dma_start(out=nat[:, h], in_=dram[h].rearrange("(i p) f -> p i f", p=P))
+            for h in range(H):
+                nc.sync.dma_start(out=q_nat[0][:, h], in_=q_pos[0, h].rearrange("(p i) f -> p i f", p=P))
+            for h in range(H):
+                nc.sync.dma_start(out=k_nat[0][:, h], in_=k_pos[0, h].rearrange("(i p) f -> p i f", p=P))
             w_rows = Wv.rearrange("(j p) k -> p j k", p=P)
             for half in range(2):
                 rows = slice(half * NW // 2, (half + 1) * NW // 2)
@@ -277,18 +278,27 @@ def tile_networklayer_pb_kernel(tc, q_pos, k_pos, x_grp, Wv, bv, out):
                 )
 
             def distances(s, h, t):
-                live = slice(t * P, B)
+                first = t * P // NT
                 column = slice(h * NT + t, h * NT + t + 1)
                 dots = banks.tile([P, B], F32, tag="bank")
+                live = dots[:, 0 : B - t * P]
                 nc.tensor.matmul(
-                    out=dots[:, live], lhsT=qkT[:, s, h, 1, t * P : (t + 1) * P], rhs=qkT[:, s, h, 0, live], start=True, stop=False
+                    out=live.rearrange("p (i x) -> p i x", i=NT),
+                    lhsT=qkT[:, s, h, 1, t * P : (t + 1) * P],
+                    rhs=qkT[:, s, h, 0].rearrange("p (i x) -> p i x", i=NT)[:, :, first:],
+                    start=True,
+                    stop=False,
                 )
                 nc.tensor.matmul(
-                    out=dots[:, live], lhsT=minus_half[:, h, :], rhs=q_extra[:, s, live], start=False, stop=True
+                    out=live.rearrange("p (i x) -> p i x", i=NT),
+                    lhsT=minus_half[:, h, :],
+                    rhs=q_extra[:, s].rearrange("p (i x) -> p i x", i=NT)[:, :, first:],
+                    start=False,
+                    stop=True,
                 )
                 nc.vector.tensor_scalar(
-                    out=logs[s][:, t, t:NT, h, :],
-                    in0=dots[:, live].rearrange("p (i b) -> p i b", b=P),
+                    out=logs[s][:, t, t:NT, h, :].rearrange("p a (x i) -> p a x i", i=NT),
+                    in0=live.rearrange("p (i a x) -> p a x i", i=NT, a=NT - t),
                     scalar1=upper[:, s, column],
                     scalar2=lower[:, s, column],
                     op0=ALU.min,

@@ -22,9 +22,12 @@ NT = B // P
 PASSES = D // (P * PACK)
 NW = D // P
 HEADS = S * H
-VECTOR_BANKS = (2, 2, 1, 1, 1, 1, 1, 1)
+VECTOR_BANKS = (1, 1, 1, 0, 0, 1, 0, 1)
 QJ = 4
 NB = 1
+SPREAD = 2
+FIRST = 1
+AHEAD = 3
 NP = 2
 NX = 3
 PIECES = 3
@@ -55,36 +58,51 @@ def tile_networklayer_pb_kernel(tc, q_pos, k_pos, x_grp, Wv, bv, out):
         work = ctx.enter_context(tc.tile_pool(name="work", bufs=2))
 
         def weights(s, i):
-            nc.scalar.activation(
-                out=w_bf[s][:, i].rearrange("p h b t -> p (h b) t")[:, :, 0 : i + 1].rearrange("p (c j) t -> p c t j", j=RUN),
-                in_=logs[s][:, 0 : i + 1, i].rearrange("p t h b -> p t (h b)").rearrange("p t (c j) -> p c t j", j=RUN),
-                func=ACT.Sigmoid,
-                scale=-0.5,
+            source = logs[s][:, 0 : i + 1, i].rearrange("p t h b -> p t (h b)")
+            target = w_bf[s][:, i].rearrange("p h b t -> p (h b) t")[:, :, 0 : i + 1]
+            if i >= SPREAD:
+                nc.scalar.activation(
+                    out=target.rearrange("p (c j) t -> p c t j", j=RUN),
+                    in_=source.rearrange("p t (c j) -> p c t j", j=RUN),
+                    func=ACT.Sigmoid,
+                    scale=-0.5,
+                )
+                return
+            packed = logs[s][:, NT - 1, i].rearrange("p h b -> p (h b)").bitcast(BF16)[:, 0 : (i + 1) * H * P]
+            packed = packed.rearrange("p (t b) -> p t b", t=i + 1)
+            nc.scalar.activation(out=packed, in_=source, func=ACT.Sigmoid, scale=-0.5)
+            nc.gpsimd.tensor_scalar(
+                out=target, in0=packed.rearrange("p t b -> p b t"), scalar1=1.0, scalar2=0.0, op0=ALU.mult, op1=ALU.add
             )
 
         def project_values(s, beside):
             v_bf = work.tile([P, NW, P, PACK], BF16, tag="v_bf", align_bytes=64)
-            for j in range(NW):
-                v_ps = banks.tile([P, NT, P], F32, tag="bank")
-                for t in range(NT):
-                    for g in range(PASSES):
-                        nc.tensor.matmul_mx(
-                            out=v_ps[:, t, :],
-                            lhsT=xw_codes[:, NW + NT * s + t, g, :].bitcast(FP8X4),
-                            lhsT_scale=xw_scales[:, NW + NT * s + t, g, :],
-                            rhs=xw_codes[:, j, g, :].bitcast(FP8X4),
-                            rhs_scale=xw_scales[:, j, g, :],
-                            start=(g == 0),
-                            stop=(g == PASSES - 1),
-                        )
-                for step in beside.get(j, []):
-                    step()
-                nc.vector.tensor_tensor(
-                    out=v_bf[:, j],
-                    in0=v_ps[:].rearrange("p t d -> p d t"),
-                    in1=bias[:, j * P : (j + 1) * P].unsqueeze(2).to_broadcast([P, P, PACK]),
-                    op=ALU.add,
-                )
+            sums = []
+            for j in range(NW + AHEAD):
+                if j < NW:
+                    v_ps = banks.tile([P, NT, P], F32, tag="bank")
+                    for t in range(NT):
+                        for g in range(PASSES):
+                            nc.tensor.matmul_mx(
+                                out=v_ps[:, t, :],
+                                lhsT=xw_codes[:, NW + NT * s + t, g, :].bitcast(FP8X4),
+                                lhsT_scale=xw_scales[:, NW + NT * s + t, g, :],
+                                rhs=xw_codes[:, j, g, :].bitcast(FP8X4),
+                                rhs_scale=xw_scales[:, j, g, :],
+                                start=(g == 0),
+                                stop=(g == PASSES - 1),
+                            )
+                    sums.append(v_ps)
+                if j >= AHEAD:
+                    done = j - AHEAD
+                    for step in beside.get(done, []):
+                        step()
+                    nc.vector.tensor_tensor(
+                        out=v_bf[:, done],
+                        in0=sums[done][:].rearrange("p t d -> p d t"),
+                        in1=bias[:, done * P : (done + 1) * P].unsqueeze(2).to_broadcast([P, P, PACK]),
+                        op=ALU.add,
+                    )
             nc.vector.quantize_mx(
                 out=v_codes[:, s, :].bitcast(FP8X4),
                 scales=v_scales[:, s, :],
@@ -337,10 +355,6 @@ def tile_networklayer_pb_kernel(tc, q_pos, k_pos, x_grp, Wv, bv, out):
                 step()
             transpose_extra_features(0)
 
-            for s in range(S):
-                for i in range(NT - 1):
-                    nc.gpsimd.memset(w_bf[s][:, i].rearrange("p h b t -> p (h b t)").bitcast(F32), 0.0)
-
             q_sums, q_calls, q_steps = statistics(q_nat[1], "q1")
             k_sums, k_calls, k_steps = statistics(k_nat[1], "k1")
             beside = {
@@ -357,13 +371,17 @@ def tile_networklayer_pb_kernel(tc, q_pos, k_pos, x_grp, Wv, bv, out):
                     transpose_positions(1)
                 if n == NX:
                     transpose_extra_features(1)
+                if n == H:
+                    for weights_of_group in w_bf:
+                        for i in range(NT - 1):
+                            nc.gpsimd.memset(weights_of_group[:, i].rearrange("p h b t -> p (h b t)").bitcast(F32), 0.0)
                 for t in range(NT):
                     logarithm(s, h, t)
                     if h == H - 1:
                         mask(s, t)
                 if n > 0:
                     quantise_rows(n - 1, row_pairs[n - 1])
-            for i in reversed(range(NT)):
+            for i in range(NT):
                 weights(0, i)
             project_values(0, {QJ: [lambda: quantise_rows(HEADS - 1, row_pairs[HEADS - 1])]})
 
@@ -380,13 +398,18 @@ def tile_networklayer_pb_kernel(tc, q_pos, k_pos, x_grp, Wv, bv, out):
                 d_cols = slice(half * 2 * DPH, (half + 1) * 2 * DPH)
                 nc.sync.dma_start(out=out[s, i * P : (i + 1) * P, d_cols], in_=o_sb[:, half, :])
 
-        for i in reversed(range(NT)):
-            weights(1, i)
-        project_values(1, {})
-        tiles = [(s, i) for s in range(S) for i in reversed(range(NT))]
-        tile_products = []
-        for n in range(len(tiles) + 1):
+
+        tiles = [(s, i) for s in range(S) for i in range(NT)]
+        products = {}
+
+        def turn(n):
+            if n < NT:
+                weights(1, n)
             if n < len(tiles):
-                tile_products.append(multiply(tiles[n][0], tiles[n][1]))
+                products[n] = multiply(tiles[n][0], tiles[n][1])
             if n > 0:
-                store(tiles[n - 1][0], tiles[n - 1][1], tile_products[n - 1], n - 1)
+                store(tiles[n - 1][0], tiles[n - 1][1], products[n - 1], n - 1)
+
+        project_values(1, {FIRST + 2 * n: [lambda n=n: turn(n)] for n in range(NT)})
+        for n in range(NT, len(tiles) + 1):
+            turn(n)

@@ -22,10 +22,10 @@ NT = B // P
 PASSES = D // (P * PACK)
 NW = D // P
 HEADS = S * H
-VECTOR_BANKS = (1, 1, 1, 0, 0, 1, 0, 1)
+VECTOR_BANKS = (2, 2, 2, 0, 1, 0, 0, 1)
 QJ = 4
 NB = 1
-SPREAD = 2
+SH = 2
 FIRST = 1
 AHEAD = 3
 NP = 2
@@ -52,27 +52,17 @@ def tile_networklayer_pb_kernel(tc, q_pos, k_pos, x_grp, Wv, bv, out):
         xw_scales = keep.tile([P, NW + S * NT, PASSES, P], U8, align_bytes=64)
         v_codes = keep.tile([P, S, D], U32, align_bytes=64)
         v_scales = keep.tile([P, S, D], U8, align_bytes=64)
-        w_bf = [keep.tile([P, NT, H, P, PACK], BF16, name="w_bf%d" % s, align_bytes=64) for s in range(S)]
+        w_bf = keep.tile([P, NT, H, P, PACK], BF16, align_bytes=64)
         logs = [keep.tile([P, NT, NT, H, P], F32, name="logs%d" % s) for s in range(S)]
 
         work = ctx.enter_context(tc.tile_pool(name="work", bufs=2))
 
         def weights(s, i):
-            source = logs[s][:, 0 : i + 1, i].rearrange("p t h b -> p t (h b)")
-            target = w_bf[s][:, i].rearrange("p h b t -> p (h b) t")[:, :, 0 : i + 1]
-            if i >= SPREAD:
-                nc.scalar.activation(
-                    out=target.rearrange("p (c j) t -> p c t j", j=RUN),
-                    in_=source.rearrange("p t (c j) -> p c t j", j=RUN),
-                    func=ACT.Sigmoid,
-                    scale=-0.5,
-                )
-                return
-            packed = logs[s][:, NT - 1, i].rearrange("p h b -> p (h b)").bitcast(BF16)[:, 0 : (i + 1) * H * P]
-            packed = packed.rearrange("p (t b) -> p t b", t=i + 1)
-            nc.scalar.activation(out=packed, in_=source, func=ACT.Sigmoid, scale=-0.5)
-            nc.gpsimd.tensor_scalar(
-                out=target, in0=packed.rearrange("p t b -> p b t"), scalar1=1.0, scalar2=0.0, op0=ALU.mult, op1=ALU.add
+            nc.scalar.activation(
+                out=w_bf[:, i].rearrange("p h b t -> p (h b) t")[:, :, 0 : i + 1].rearrange("p (c j) t -> p c t j", j=RUN),
+                in_=logs[s][:, 0 : i + 1, i].rearrange("p t h b -> p t (h b)").rearrange("p t (c j) -> p c t j", j=RUN),
+                func=ACT.Sigmoid,
+                scale=-0.5,
             )
 
         def project_values(s, beside):
@@ -115,7 +105,7 @@ def tile_networklayer_pb_kernel(tc, q_pos, k_pos, x_grp, Wv, bv, out):
             nc.vector.quantize_mx(
                 out=w_codes[:].rearrange("p h b -> p (h b)").bitcast(FP8X4),
                 scales=w_scales[:].rearrange("p h b -> p (h b)"),
-                in_=w_bf[s][:, i].rearrange("p h b t -> p (h b t)"),
+                in_=w_bf[:, i].rearrange("p h b t -> p (h b t)"),
             )
             products = []
             for pair in range(H // 2):
@@ -187,28 +177,38 @@ def tile_networklayer_pb_kernel(tc, q_pos, k_pos, x_grp, Wv, bv, out):
                 op0=ALU.mult,
             )
 
+            for i in range(NT - 1):
+                nc.vector.memset(w_bf[:, i].rearrange("p h b t -> p (h b t)").bitcast(F32), 0.0)
+
             qkT = inputs.tile([P, S, H, 2, B], BF16)
             q_extra = inputs.tile([P, S, B], BF16)
             k_squares = inputs.tile([P, S, H * NT], F32)
             upper = inputs.tile([P, S, H * NT], F32)
             lower = inputs.tile([P, S, H * NT], F32)
 
-            def statistics(nat, name):
-                stats = inputs.tile([P, H * NT, 3], F32, name=name + "_stats")
-                part = inputs.tile([P, H * NT], F32, name=name + "_part")
-                sums = inputs.tile([P, H * NT], F32, name=name + "_sums")
+            def statistics(nat, sums, first, last, name):
+                n = (last - first) * NT
+                stats = inputs.tile([P, n, 3], F32, name=name + "_stats")
+                part = inputs.tile([P, n], F32, name=name + "_part")
                 by_call = stats[:].rearrange("p (c e) k -> p c (e k)", e=2)
-                pairs = nat[:].rearrange("p h (c e) f -> p (h c) f e", e=2)
-                calls = [
-                    lambda c=c: nc.vector.bn_stats(out=by_call[:, c, :], in_=pairs[:, c]) for c in range(H * NT // 2)
-                ]
+                pairs = nat[:, first:last].rearrange("p h (c e) f -> p (h c) f e", e=2)
+                calls = [lambda c=c: nc.vector.bn_stats(out=by_call[:, c, :], in_=pairs[:, c]) for c in range(n // 2)]
                 steps = [
                     lambda: nc.vector.scalar_tensor_tensor(
                         out=part[:], in0=stats[:, :, 1], scalar=float(DPP), in1=stats[:, :, 1], op0=ALU.mult, op1=ALU.mult
                     ),
-                    lambda: nc.vector.tensor_tensor(out=sums[:], in0=stats[:, :, 2], in1=part[:], op=ALU.add),
+                    lambda: nc.vector.tensor_tensor(
+                        out=sums[:, first * NT : last * NT], in0=stats[:, :, 2], in1=part[:], op=ALU.add
+                    ),
                 ]
-                return sums, calls, steps
+                return calls, steps
+
+            def scalar_statistics(nat, sums, last):
+                squares = inputs.tile([P, last * NT, DPP], BF16)
+                for c in range(last * NT):
+                    nc.scalar.activation(
+                        out=squares[:, c], in_=nat[:, c // NT, c % NT, :], func=ACT.Square, accum_out=sums[:, c : c + 1]
+                    )
 
             def query_pieces(s, sums, engine):
                 pieces = q_feat[s][:, :, 0 : H * PIECES].rearrange("p i (h j) -> p i h j", j=PIECES)
@@ -221,26 +221,27 @@ def tile_networklayer_pb_kernel(tc, q_pos, k_pos, x_grp, Wv, bv, out):
                     lambda: engine.tensor_tensor(out=pieces[:, :, :, 2], in0=left[:], in1=pieces[:, :, :, 1], op=ALU.subtract),
                 ]
 
-            def key_columns(s, sums):
+            def key_columns(s, sums, first, last):
+                columns = slice(first * NT, last * NT)
                 return [
                     lambda: nc.gpsimd.tensor_scalar(
-                        out=upper[:, s, :],
-                        in0=sums[:],
+                        out=upper[:, s, columns],
+                        in0=sums[:, columns],
                         scalar1=D2_FLOOR,
                         scalar2=0.5 * (1.0 - CANCELLED),
                         op0=ALU.add,
                         op1=ALU.mult,
                     ),
                     lambda: nc.gpsimd.tensor_scalar(
-                        out=lower[:, s, :],
-                        in0=sums[:],
+                        out=lower[:, s, columns],
+                        in0=sums[:, columns],
                         scalar1=0.5,
                         scalar2=0.5 * D2_CEIL,
                         op0=ALU.mult,
                         op1=ALU.subtract,
                     ),
                     lambda: nc.gpsimd.tensor_scalar(
-                        out=k_squares[:, s, :], in0=sums[:], scalar1=D2_FLOOR, scalar2=None, op0=ALU.add
+                        out=k_squares[:, s, columns], in0=sums[:, columns], scalar1=D2_FLOOR, scalar2=None, op0=ALU.add
                     ),
                 ]
 
@@ -257,8 +258,8 @@ def tile_networklayer_pb_kernel(tc, q_pos, k_pos, x_grp, Wv, bv, out):
                     nc.tensor.transpose(tp[:, i, :], blocks[:, i, :], ident_bf[:])
                 return tp[:].rearrange("p i b -> p (i b)")
 
-            def transpose_positions(s):
-                for h in range(H):
+            def transpose_positions(s, heads):
+                for h in heads:
                     tp = banks.tile([P, 2, NT, P], BF16, tag="bank")
                     for i in range(NT):
                         nc.tensor.transpose(tp[:, 0, i, :], q_nat[s][:, h, i, :], ident_bf[:])
@@ -345,22 +346,27 @@ def tile_networklayer_pb_kernel(tc, q_pos, k_pos, x_grp, Wv, bv, out):
                     channel_multiplier=-1,
                 )
 
-            q_sums, q_calls, q_steps = statistics(q_nat[0], "q0")
-            transpose_positions(0)
-            k_sums, k_calls, k_steps = statistics(k_nat[0], "k0")
+            q_sums = [inputs.tile([P, H * NT], F32, name="q_sums%d" % s) for s in range(S)]
+            k_sums = [inputs.tile([P, H * NT], F32, name="k_sums%d" % s) for s in range(S)]
+            scalar_statistics(q_nat[0], q_sums[0], SH)
+            q_calls, q_steps = statistics(q_nat[0], q_sums[0], SH, H, "q0")
+            early_calls, early_steps = statistics(k_nat[0], k_sums[0], 0, H // 2, "k0_early")
+            late_calls, late_steps = statistics(k_nat[0], k_sums[0], H // 2, H, "k0_late")
             for call in q_calls:
                 call()
-            run_in_turns(k_calls, q_steps + query_pieces(0, q_sums, nc.vector))
-            for step in k_steps + key_columns(0, k_sums):
-                step()
+            run_in_turns(early_calls, q_steps + query_pieces(0, q_sums[0], nc.vector))
+            transpose_positions(0, range(H // 2))
             transpose_extra_features(0)
+            transpose_positions(0, range(H // 2, H))
+            run_in_turns(late_calls, early_steps + key_columns(0, k_sums[0], 0, H // 2))
 
-            q_sums, q_calls, q_steps = statistics(q_nat[1], "q1")
-            k_sums, k_calls, k_steps = statistics(k_nat[1], "k1")
+            q_calls, q_steps = statistics(q_nat[1], q_sums[1], 0, H, "q1")
+            k_calls, k_steps = statistics(k_nat[1], k_sums[1], 0, H, "k1")
             beside = {
+                0: late_steps + key_columns(0, k_sums[0], H // 2, H),
                 NB: q_calls,
                 NB + 1: q_steps + k_calls,
-                NB + 2: query_pieces(1, q_sums, nc.gpsimd) + k_steps + key_columns(1, k_sums),
+                NB + 2: query_pieces(1, q_sums[1], nc.gpsimd) + k_steps + key_columns(1, k_sums[1], 0, H),
             }
             row_pairs = []
             for n in range(HEADS):
@@ -368,20 +374,16 @@ def tile_networklayer_pb_kernel(tc, q_pos, k_pos, x_grp, Wv, bv, out):
                 run_in_turns([lambda t=t: distances(s, h, t) for t in range(NT)], beside.get(n, []))
                 row_pairs.append(transpose_rows(n))
                 if n == NP:
-                    transpose_positions(1)
+                    transpose_positions(1, range(H))
                 if n == NX:
                     transpose_extra_features(1)
-                if n == H:
-                    for weights_of_group in w_bf:
-                        for i in range(NT - 1):
-                            nc.gpsimd.memset(weights_of_group[:, i].rearrange("p h b t -> p (h b t)").bitcast(F32), 0.0)
                 for t in range(NT):
                     logarithm(s, h, t)
                     if h == H - 1:
                         mask(s, t)
                 if n > 0:
                     quantise_rows(n - 1, row_pairs[n - 1])
-            for i in range(NT):
+            for i in reversed(range(NT)):
                 weights(0, i)
             project_values(0, {QJ: [lambda: quantise_rows(HEADS - 1, row_pairs[HEADS - 1])]})
 
@@ -399,14 +401,14 @@ def tile_networklayer_pb_kernel(tc, q_pos, k_pos, x_grp, Wv, bv, out):
                 nc.sync.dma_start(out=out[s, i * P : (i + 1) * P, d_cols], in_=o_sb[:, half, :])
 
 
-        tiles = [(s, i) for s in range(S) for i in range(NT)]
+        tiles = [(s, i) for s in range(S) for i in reversed(range(NT))]
         products = {}
 
         def turn(n):
-            if n < NT:
-                weights(1, n)
             if n < len(tiles):
                 products[n] = multiply(tiles[n][0], tiles[n][1])
+            if n < NT:
+                weights(1, tiles[n][1])
             if n > 0:
                 store(tiles[n - 1][0], tiles[n - 1][1], products[n - 1], n - 1)
 

@@ -25,7 +25,7 @@ HEADS = S * H
 VECTOR_BANKS = (2, 2, 2, 0, 1, 0, 0, 1)
 QJ = 4
 NB = 1
-SH = 2
+VECTOR_ZEROS = 2
 FIRST = 1
 AHEAD = 3
 NP = 2
@@ -177,8 +177,11 @@ def tile_networklayer_pb_kernel(tc, q_pos, k_pos, x_grp, Wv, bv, out):
                 op0=ALU.mult,
             )
 
-            for i in range(NT - 1):
-                nc.vector.memset(w_bf[:, i].rearrange("p h b t -> p (h b t)").bitcast(F32), 0.0)
+            def zero_weights(tiles, engine):
+                for i in tiles:
+                    engine.memset(w_bf[:, i].rearrange("p h b t -> p (h b t)").bitcast(F32), 0.0)
+
+            zero_weights(range(VECTOR_ZEROS), nc.vector)
 
             qkT = inputs.tile([P, S, H, 2, B], BF16)
             q_extra = inputs.tile([P, S, B], BF16)
@@ -186,29 +189,22 @@ def tile_networklayer_pb_kernel(tc, q_pos, k_pos, x_grp, Wv, bv, out):
             upper = inputs.tile([P, S, H * NT], F32)
             lower = inputs.tile([P, S, H * NT], F32)
 
-            def statistics(nat, sums, first, last, name):
-                n = (last - first) * NT
-                stats = inputs.tile([P, n, 3], F32, name=name + "_stats")
-                part = inputs.tile([P, n], F32, name=name + "_part")
+            def statistics(nat, name):
+                stats = inputs.tile([P, H * NT, 3], F32, name=name + "_stats")
+                part = inputs.tile([P, H * NT], F32, name=name + "_part")
+                sums = inputs.tile([P, H * NT], F32, name=name + "_sums")
                 by_call = stats[:].rearrange("p (c e) k -> p c (e k)", e=2)
-                pairs = nat[:, first:last].rearrange("p h (c e) f -> p (h c) f e", e=2)
-                calls = [lambda c=c: nc.vector.bn_stats(out=by_call[:, c, :], in_=pairs[:, c]) for c in range(n // 2)]
+                pairs = nat[:].rearrange("p h (c e) f -> p (h c) f e", e=2)
+                calls = [
+                    lambda c=c: nc.vector.bn_stats(out=by_call[:, c, :], in_=pairs[:, c]) for c in range(H * NT // 2)
+                ]
                 steps = [
                     lambda: nc.vector.scalar_tensor_tensor(
                         out=part[:], in0=stats[:, :, 1], scalar=float(DPP), in1=stats[:, :, 1], op0=ALU.mult, op1=ALU.mult
                     ),
-                    lambda: nc.vector.tensor_tensor(
-                        out=sums[:, first * NT : last * NT], in0=stats[:, :, 2], in1=part[:], op=ALU.add
-                    ),
+                    lambda: nc.vector.tensor_tensor(out=sums[:], in0=stats[:, :, 2], in1=part[:], op=ALU.add),
                 ]
-                return calls, steps
-
-            def scalar_statistics(nat, sums, last):
-                squares = inputs.tile([P, last * NT, DPP], BF16)
-                for c in range(last * NT):
-                    nc.scalar.activation(
-                        out=squares[:, c], in_=nat[:, c // NT, c % NT, :], func=ACT.Square, accum_out=sums[:, c : c + 1]
-                    )
+                return sums, calls, steps
 
             def query_pieces(s, sums, engine):
                 pieces = q_feat[s][:, :, 0 : H * PIECES].rearrange("p i (h j) -> p i h j", j=PIECES)
@@ -221,27 +217,26 @@ def tile_networklayer_pb_kernel(tc, q_pos, k_pos, x_grp, Wv, bv, out):
                     lambda: engine.tensor_tensor(out=pieces[:, :, :, 2], in0=left[:], in1=pieces[:, :, :, 1], op=ALU.subtract),
                 ]
 
-            def key_columns(s, sums, first, last):
-                columns = slice(first * NT, last * NT)
+            def key_columns(s, sums):
                 return [
                     lambda: nc.gpsimd.tensor_scalar(
-                        out=upper[:, s, columns],
-                        in0=sums[:, columns],
+                        out=upper[:, s, :],
+                        in0=sums[:],
                         scalar1=D2_FLOOR,
                         scalar2=0.5 * (1.0 - CANCELLED),
                         op0=ALU.add,
                         op1=ALU.mult,
                     ),
                     lambda: nc.gpsimd.tensor_scalar(
-                        out=lower[:, s, columns],
-                        in0=sums[:, columns],
+                        out=lower[:, s, :],
+                        in0=sums[:],
                         scalar1=0.5,
                         scalar2=0.5 * D2_CEIL,
                         op0=ALU.mult,
                         op1=ALU.subtract,
                     ),
                     lambda: nc.gpsimd.tensor_scalar(
-                        out=k_squares[:, s, columns], in0=sums[:, columns], scalar1=D2_FLOOR, scalar2=None, op0=ALU.add
+                        out=k_squares[:, s, :], in0=sums[:], scalar1=D2_FLOOR, scalar2=None, op0=ALU.add
                     ),
                 ]
 
@@ -258,8 +253,8 @@ def tile_networklayer_pb_kernel(tc, q_pos, k_pos, x_grp, Wv, bv, out):
                     nc.tensor.transpose(tp[:, i, :], blocks[:, i, :], ident_bf[:])
                 return tp[:].rearrange("p i b -> p (i b)")
 
-            def transpose_positions(s, heads):
-                for h in heads:
+            def transpose_positions(s):
+                for h in range(H):
                     tp = banks.tile([P, 2, NT, P], BF16, tag="bank")
                     for i in range(NT):
                         nc.tensor.transpose(tp[:, 0, i, :], q_nat[s][:, h, i, :], ident_bf[:])
@@ -346,27 +341,24 @@ def tile_networklayer_pb_kernel(tc, q_pos, k_pos, x_grp, Wv, bv, out):
                     channel_multiplier=-1,
                 )
 
-            q_sums = [inputs.tile([P, H * NT], F32, name="q_sums%d" % s) for s in range(S)]
-            k_sums = [inputs.tile([P, H * NT], F32, name="k_sums%d" % s) for s in range(S)]
-            scalar_statistics(q_nat[0], q_sums[0], SH)
-            q_calls, q_steps = statistics(q_nat[0], q_sums[0], SH, H, "q0")
-            early_calls, early_steps = statistics(k_nat[0], k_sums[0], 0, H // 2, "k0_early")
-            late_calls, late_steps = statistics(k_nat[0], k_sums[0], H // 2, H, "k0_late")
+            q_sums, q_calls, q_steps = statistics(q_nat[0], "q0")
+            transpose_positions(0)
+            k_sums, k_calls, k_steps = statistics(k_nat[0], "k0")
             for call in q_calls:
                 call()
-            run_in_turns(early_calls, q_steps + query_pieces(0, q_sums[0], nc.vector))
-            transpose_positions(0, range(H // 2))
+            run_in_turns(k_calls, q_steps + query_pieces(0, q_sums, nc.vector))
+            for step in k_steps + key_columns(0, k_sums):
+                step()
             transpose_extra_features(0)
-            transpose_positions(0, range(H // 2, H))
-            run_in_turns(late_calls, early_steps + key_columns(0, k_sums[0], 0, H // 2))
 
-            q_calls, q_steps = statistics(q_nat[1], q_sums[1], 0, H, "q1")
-            k_calls, k_steps = statistics(k_nat[1], k_sums[1], 0, H, "k1")
+            zero_weights(range(VECTOR_ZEROS, NT - 1), nc.gpsimd)
+
+            q_sums, q_calls, q_steps = statistics(q_nat[1], "q1")
+            k_sums, k_calls, k_steps = statistics(k_nat[1], "k1")
             beside = {
-                0: late_steps + key_columns(0, k_sums[0], H // 2, H),
                 NB: q_calls,
                 NB + 1: q_steps + k_calls,
-                NB + 2: query_pieces(1, q_sums[1], nc.gpsimd) + k_steps + key_columns(1, k_sums[1], 0, H),
+                NB + 2: query_pieces(1, q_sums, nc.gpsimd) + k_steps + key_columns(1, k_sums),
             }
             row_pairs = []
             for n in range(HEADS):
@@ -374,7 +366,7 @@ def tile_networklayer_pb_kernel(tc, q_pos, k_pos, x_grp, Wv, bv, out):
                 run_in_turns([lambda t=t: distances(s, h, t) for t in range(NT)], beside.get(n, []))
                 row_pairs.append(transpose_rows(n))
                 if n == NP:
-                    transpose_positions(1, range(H))
+                    transpose_positions(1)
                 if n == NX:
                     transpose_extra_features(1)
                 for t in range(NT):

from contextlib import ExitStack

import concourse.mybir as mybir
from concourse.masks import make_identity

F32 = mybir.dt.float32
BF16 = mybir.dt.bfloat16
U32 = mybir.dt.uint32
U8 = mybir.dt.uint8
FP8X4 = mybir.dt.float8_e4m3fn_x4
ALU = mybir.AluOpType
ACT = mybir.ActivationFunctionType
AX = mybir.AxisListType

P = 128
PACK = 4
S, H, B = 2, 4, 512
DPP = 128
D = 1024
DPH = D // H
NT = B // P
PASSES = D // (P * PACK)
NW = D // P
HEADS = S * H
VECTOR_BANKS = (2, 2, 2, 0, 1, 0, 0, 1)
QJ = 4
NB = 1
VECTOR_ZEROS = 2
FIRST = 1
AHEAD = 3
NP = 2
NX = 3
PIECES = 3
D2_FLOOR = 1e-12
D2_CEIL = 2.0**64
CANCELLED = 2.0**-22
RUN = 4
MASKED_LOG = 1e30

FLOPS = 2 * S * B * D * D + 2 * S * H * B * B * DPP + 2 * S * H * B * B * DPH


def tile_networklayer_pb_kernel(tc, q_pos, k_pos, x_grp, Wv, bv, out):
    nc = tc.nc
    with ExitStack() as ctx:
        keep = ctx.enter_context(tc.tile_pool(name="keep", bufs=1))
        banks = ctx.enter_context(tc.psum_pool(name="banks", bufs=8))
        ctx.enter_context(tc.manual_schedule())

        bias = keep.tile([P, D], BF16)
        xw_codes = keep.tile([P, NW + S * NT, PASSES, P], U32, align_bytes=64)
        xw_scales = keep.tile([P, NW + S * NT, PASSES, P], U8, align_bytes=64)
        v_codes = keep.tile([P, S, D], U32, align_bytes=64)
        v_scales = keep.tile([P, S, D], U8, align_bytes=64)
        w_bf = keep.tile([P, NT, H, P, PACK], BF16, align_bytes=64)
        logs = [keep.tile([P, NT, NT, H, P], F32, name="logs%d" % s) for s in range(S)]

        work = ctx.enter_context(tc.tile_pool(name="work", bufs=2))

        def weights(s, i):
            nc.scalar.activation(
                out=w_bf[:, i].rearrange("p h b t -> p (h b) t")[:, :, 0 : i + 1].rearrange("p (c j) t -> p c t j", j=RUN),
                in_=logs[s][:, 0 : i + 1, i].rearrange("p t h b -> p t (h b)").rearrange("p t (c j) -> p c t j", j=RUN),
                func=ACT.Sigmoid,
                scale=-0.5,
            )

        def project_values(s, beside):
            v_bf = work.tile([P, NW, P, PACK], BF16, tag="v_bf", align_bytes=64)
            sums = []
            for j in range(NW + AHEAD):
                if j < NW:
                    v_ps = banks.tile([P, NT, P], F32, tag="bank")
                    for t in range(NT):
                        for g in range(PASSES):
                            nc.tensor.matmul_mx(
                                out=v_ps[:, t, :],
                                lhsT=xw_codes[:, NW + NT * s + t, g, :].bitcast(FP8X4),
                                lhsT_scale=xw_scales[:, NW + NT * s + t, g, :],
                                rhs=xw_codes[:, j, g, :].bitcast(FP8X4),
                                rhs_scale=xw_scales[:, j, g, :],
                                start=(g == 0),
                                stop=(g == PASSES - 1),
                            )
                    sums.append(v_ps)
                if j >= AHEAD:
                    done = j - AHEAD
                    for step in beside.get(done, []):
                        step()
                    nc.vector.tensor_tensor(
                        out=v_bf[:, done],
                        in0=sums[done][:].rearrange("p t d -> p d t"),
                        in1=bias[:, done * P : (done + 1) * P].unsqueeze(2).to_broadcast([P, P, PACK]),
                        op=ALU.add,
                    )
            nc.vector.quantize_mx(
                out=v_codes[:, s, :].bitcast(FP8X4),
                scales=v_scales[:, s, :],
                in_=v_bf[:].rearrange("p j d t -> p (j d t)"),
            )

        def multiply(s, i):
            w_codes = work.tile([P, H, P], U32, tag="w_codes", align_bytes=64)
            w_scales = work.tile([P, H, P], U8, tag="w_scales", align_bytes=64)
            nc.vector.quantize_mx(
                out=w_codes[:].rearrange("p h b -> p (h b)").bitcast(FP8X4),
                scales=w_scales[:].rearrange("p h b -> p (h b)"),
                in_=w_bf[:, i].rearrange("p h b t -> p (h b t)"),
            )
            products = []
            for pair in range(H // 2):
                o_ps = banks.tile([P, 2, DPH], F32, tag="bank")
                for e in range(2):
                    h = 2 * pair + e
                    d_cols = slice(h * DPH, (h + 1) * DPH)
                    nc.tensor.matmul_mx(
                        out=o_ps[:, e, :],
                        lhsT=w_codes[:, h, :].bitcast(FP8X4),
                        lhsT_scale=w_scales[:, h, :],
                        rhs=v_codes[:, s, d_cols].bitcast(FP8X4),
                        rhs_scale=v_scales[:, s, d_cols],
                        start=True,
                        stop=True,
                    )
                products.append(o_ps)
            return products

        with ExitStack() as part_one:
            inputs = part_one.enter_context(tc.tile_pool(name="inputs", bufs=1))
            stage = part_one.enter_context(tc.tile_pool(name="stage", bufs=3))
            q_nat = [inputs.tile([P, H, NT, DPP], BF16, name="q_nat%d" % s) for s in range(S)]
            k_nat = [inputs.tile([P, H, NT, DPP], BF16, name="k_nat%d" % s) for s in range(S)]
            w_nat = inputs.tile([P, NW, D], BF16)
            x_nat = [inputs.tile([P, NT, D], BF16, name="x_nat%d" % s) for s in range(S)]

            def load_positions(s):
                nc.sync.dma_start(out=q_nat[s][:], in_=q_pos[s].rearrange("h (p i) f -> p h i f", p=P))
                nc.sync.dma_start(out=k_nat[s][:], in_=k_pos[s].rearrange("h (i p) f -> p h i f", p=P))

            for h in range(H):
                nc.sync.dma_start(out=q_nat[0][:, h], in_=q_pos[0, h].rearrange("(p i) f -> p i f", p=P))
            for h in range(H):
                nc.sync.dma_start(out=k_nat[0][:, h], in_=k_pos[0, h].rearrange("(i p) f -> p i f", p=P))
            w_rows = Wv.rearrange("(j p) k -> p j k", p=P)
            for half in range(2):
                rows = slice(half * NW // 2, (half + 1) * NW // 2)
                nc.sync.dma_start(out=w_nat[:, rows, :], in_=w_rows[:, rows, :])
                if half == 0:
                    load_positions(1)
            for s in range(S):
                nc.sync.dma_start(out=x_nat[s][:], in_=x_grp[s].rearrange("(t p) k -> p t k", p=P))
            nc.sync.dma_start(out=bias[:], in_=bv.partition_broadcast(P))

            ident_bf = inputs.tile([P, P], BF16)
            make_identity(nc, ident_bf[:])
            ident_f32 = inputs.tile([P, P], F32)
            make_identity(nc, ident_f32[:])
            one = inputs.tile([P, 1], F32)
            nc.vector.memset(one[:], 1.0)
            nc.scalar.activation(out=one[:], in_=one[:], func=ACT.Ln)
            q_feat = [inputs.tile([P, NT, P], BF16, name="q_feat%d" % s) for s in range(S)]
            for s in range(S):
                nc.vector.memset(q_feat[s][:], 0.0)
            head_rows = inputs.tile([P, H], F32)
            nc.vector.tensor_reduce(
                out=head_rows[:],
                in_=ident_f32[:, 0 : H * PIECES].rearrange("p (h j) -> p h j", j=PIECES),
                axis=AX.X,
                op=ALU.add,
            )
            minus_half = inputs.tile([P, H, P], BF16)
            nc.vector.tensor_scalar(
                out=minus_half[:],
                in0=head_rows[:].unsqueeze(2).to_broadcast([P, H, P]),
                scalar1=-0.5,
                scalar2=None,
                op0=ALU.mult,
            )

            def zero_weights(tiles, engine):
                for i in tiles:
                    engine.memset(w_bf[:, i].rearrange("p h b t -> p (h b t)").bitcast(F32), 0.0)

            zero_weights(range(VECTOR_ZEROS), nc.vector)

            qkT = inputs.tile([P, S, H, 2, B], BF16)
            q_extra = inputs.tile([P, S, B], BF16)
            k_squares = inputs.tile([P, S, H * NT], F32)
            upper = inputs.tile([P, S, H * NT], F32)
            lower = inputs.tile([P, S, H * NT], F32)

            def statistics(nat, name):
                stats = inputs.tile([P, H * NT, 3], F32, name=name + "_stats")
                part = inputs.tile([P, H * NT], F32, name=name + "_part")
                sums = inputs.tile([P, H * NT], F32, name=name + "_sums")
                by_call = stats[:].rearrange("p (c e) k -> p c (e k)", e=2)
                pairs = nat[:].rearrange("p h (c e) f -> p (h c) f e", e=2)
                calls = [
                    lambda c=c: nc.vector.bn_stats(out=by_call[:, c, :], in_=pairs[:, c]) for c in range(H * NT // 2)
                ]
                steps = [
                    lambda: nc.vector.scalar_tensor_tensor(
                        out=part[:], in0=stats[:, :, 1], scalar=float(DPP), in1=stats[:, :, 1], op0=ALU.mult, op1=ALU.mult
                    ),
                    lambda: nc.vector.tensor_tensor(out=sums[:], in0=stats[:, :, 2], in1=part[:], op=ALU.add),
                ]
                return sums, calls, steps

            def query_pieces(s, sums, engine):
                pieces = q_feat[s][:, :, 0 : H * PIECES].rearrange("p i (h j) -> p i h j", j=PIECES)
                whole = sums[:].rearrange("p (h i) -> p i h", i=NT)
                left = inputs.tile([P, NT, H], F32, name="left%d" % s)
                return [
                    lambda: engine.tensor_copy(out=pieces[:, :, :, 0], in_=whole),
                    lambda: engine.tensor_tensor(out=left[:], in0=whole, in1=pieces[:, :, :, 0], op=ALU.subtract),
                    lambda: engine.tensor_tensor(out=pieces[:, :, :, 1], in0=whole, in1=pieces[:, :, :, 0], op=ALU.subtract),
                    lambda: engine.tensor_tensor(out=pieces[:, :, :, 2], in0=left[:], in1=pieces[:, :, :, 1], op=ALU.subtract),
                ]

            def key_columns(s, sums):
                return [
                    lambda: nc.gpsimd.tensor_scalar(
                        out=upper[:, s, :],
                        in0=sums[:],
                        scalar1=D2_FLOOR,
                        scalar2=0.5 * (1.0 - CANCELLED),
                        op0=ALU.add,
                        op1=ALU.mult,
                    ),
                    lambda: nc.gpsimd.tensor_scalar(
                        out=lower[:, s, :],
                        in0=sums[:],
                        scalar1=0.5,
                        scalar2=0.5 * D2_CEIL,
                        op0=ALU.mult,
                        op1=ALU.subtract,
                    ),
                    lambda: nc.gpsimd.tensor_scalar(
                        out=k_squares[:, s, :], in0=sums[:], scalar1=D2_FLOOR, scalar2=None, op0=ALU.add
                    ),
                ]

            def run_in_turns(calls, steps):
                for n in range(max(len(calls), len(steps))):
                    if n < len(calls):
                        calls[n]()
                    if n < len(steps):
                        steps[n]()

            def transposed(blocks):
                tp = banks.tile([P, NT, P], BF16, tag="bank")
                for i in range(NT):
                    nc.tensor.transpose(tp[:, i, :], blocks[:, i, :], ident_bf[:])
                return tp[:].rearrange("p i b -> p (i b)")

            def transpose_positions(s):
                for h in range(H):
                    tp = banks.tile([P, 2, NT, P], BF16, tag="bank")
                    for i in range(NT):
                        nc.tensor.transpose(tp[:, 0, i, :], q_nat[s][:, h, i, :], ident_bf[:])
                    for i in range(NT):
                        nc.tensor.transpose(tp[:, 1, i, :], k_nat[s][:, h, i, :], ident_bf[:])
                    nc.scalar.copy(out=qkT[:, s, h], in_=tp[:].rearrange("p x i b -> p x (i b)"))

            def transpose_extra_features(s):
                nc.scalar.copy(out=q_extra[:, s, :], in_=transposed(q_feat[s]))

            def row_tile(n):
                if n < NW:
                    return w_nat[:, n, :]
                return x_nat[(n - NW) // NT][:, (n - NW) % NT, :]

            def transpose_rows(pair):
                grouped = stage.tile([P, 2 * PASSES * P * PACK], BF16, tag="grouped", align_bytes=64)
                words = grouped[:].bitcast(F32).rearrange("p (n g r u) -> p n g r u", n=2, g=PASSES, u=2)
                for n in range(2):
                    source = row_tile(2 * pair + n).bitcast(F32)
                    tp = banks.tile([P, PASSES, 2, P], F32, tag="bank")
                    for g in range(PASSES):
                        for u in range(2):
                            first = (2 * g + u) * P
                            nc.tensor.transpose(tp[:, g, u, :], source[:, first : first + P], ident_f32[:])
                    nc.scalar.copy(out=words[:, n], in_=tp[:].rearrange("p g u r -> p g r u"))
                return grouped

            def quantise_rows(pair, grouped):
                tiles = slice(2 * pair, 2 * pair + 2)
                nc.vector.quantize_mx(
                    out=xw_codes[:, tiles].rearrange("p n g r -> p (n g r)").bitcast(FP8X4),
                    scales=xw_scales[:, tiles].rearrange("p n g r -> p (n g r)"),
                    in_=grouped[:],
                )

            def distances(s, h, t):
                first = t * P // NT
                column = slice(h * NT + t, h * NT + t + 1)
                dots = banks.tile([P, B], F32, tag="bank")
                live = dots[:, 0 : B - t * P]
                nc.tensor.matmul(
                    out=live.rearrange("p (i x) -> p i x", i=NT),
                    lhsT=qkT[:, s, h, 1, t * P : (t + 1) * P],
                    rhs=qkT[:, s, h, 0].rearrange("p (i x) -> p i x", i=NT)[:, :, first:],
                    start=True,
                    stop=False,
                )
                nc.tensor.matmul(
                    out=live.rearrange("p (i x) -> p i x", i=NT),
                    lhsT=minus_half[:, h, :],
                    rhs=q_extra[:, s].rearrange("p (i x) -> p i x", i=NT)[:, :, first:],
                    start=False,
                    stop=True,
                )
                nc.vector.tensor_scalar(
                    out=logs[s][:, t, t:NT, h, :].rearrange("p a (x i) -> p a x i", i=NT),
                    in0=live.rearrange("p (i a x) -> p a x i", i=NT, a=NT - t),
                    scalar1=upper[:, s, column],
                    scalar2=lower[:, s, column],
                    op0=ALU.min,
                    op1=ALU.max,
                )

            def logarithm(s, h, t):
                logd = logs[s][:, t, t:NT, h, :]
                nc.scalar.activation(
                    out=logd,
                    in_=logd,
                    func=ACT.Ln,
                    scale=-2.0,
                    bias=k_squares[:, s, h * NT + t : h * NT + t + 1],
                )

            def mask(s, t):
                diagonal = logs[s][:, t, t]
                nc.gpsimd.affine_select(
                    out=diagonal,
                    in_=diagonal,
                    pattern=[[0, H], [1, P]],
                    compare_op=ALU.is_ge,
                    fill=MASKED_LOG,
                    base=0,
                    channel_multiplier=-1,
                )

            q_sums, q_calls, q_steps = statistics(q_nat[0], "q0")
            transpose_positions(0)
            k_sums, k_calls, k_steps = statistics(k_nat[0], "k0")
            for call in q_calls:
                call()
            run_in_turns(k_calls, q_steps + query_pieces(0, q_sums, nc.vector))
            for step in k_steps + key_columns(0, k_sums):
                step()
            transpose_extra_features(0)

            zero_weights(range(VECTOR_ZEROS, NT - 1), nc.gpsimd)

            q_sums, q_calls, q_steps = statistics(q_nat[1], "q1")
            k_sums, k_calls, k_steps = statistics(k_nat[1], "k1")
            beside = {
                NB: q_calls,
                NB + 1: q_steps + k_calls,
                NB + 2: query_pieces(1, q_sums, nc.gpsimd) + k_steps + key_columns(1, k_sums),
            }
            row_pairs = []
            for n in range(HEADS):
                s, h = n // H, n % H
                run_in_turns([lambda t=t: distances(s, h, t) for t in range(NT)], beside.get(n, []))
                row_pairs.append(transpose_rows(n))
                if n == NP:
                    transpose_positions(1)
                if n == NX:
                    transpose_extra_features(1)
                for t in range(NT):
                    logarithm(s, h, t)
                    if h == H - 1:
                        mask(s, t)
                if n > 0:
                    quantise_rows(n - 1, row_pairs[n - 1])
            for i in reversed(range(NT)):
                weights(0, i)
            project_values(0, {QJ: [lambda: quantise_rows(HEADS - 1, row_pairs[HEADS - 1])]})

        outputs = ctx.enter_context(tc.tile_pool(name="outputs", bufs=HEADS))

        def store(s, i, products, n):
            o_sb = outputs.tile([P, H // 2, 2 * DPH], F32, tag="o_sb")
            for half in range(2):
                source = products[half][:].rearrange("p e d -> p (e d)")
                if half >= VECTOR_BANKS[n]:
                    nc.scalar.copy(out=o_sb[:, half, :], in_=source)
                else:
                    nc.vector.tensor_copy(out=o_sb[:, half, :], in_=source)
                d_cols = slice(half * 2 * DPH, (half + 1) * 2 * DPH)
                nc.sync.dma_start(out=out[s, i * P : (i + 1) * P, d_cols], in_=o_sb[:, half, :])


        tiles = [(s, i) for s in range(S) for i in reversed(range(NT))]
        products = {}

        def turn(n):
            if n < len(tiles):
                products[n] = multiply(tiles[n][0], tiles[n][1])
            if n < NT:
                weights(1, tiles[n][1])
            if n > 0:
                store(tiles[n - 1][0], tiles[n - 1][1], products[n - 1], n - 1)

        project_values(1, {FIRST + 2 * n: [lambda n=n: turn(n)] for n in range(NT)})
        for n in range(NT, len(tiles) + 1):
            turn(n)
